import numpy as np
import ml_dtypes


def mxq(x, axis, fmt="e4m3"):
    dtype, down = {"e4m3": (ml_dtypes.float8_e4m3fn, 7), "e5m2": (ml_dtypes.float8_e5m2, 14)}[fmt]
    v = np.moveaxis(np.asarray(x, np.float32).astype(ml_dtypes.bfloat16).astype(np.float64), axis, -1)
    blocks = v.reshape(v.shape[:-1] + (-1, 32))
    amax = np.abs(blocks).max(-1, keepdims=True)
    byte = np.maximum(np.where(amax > 0, np.frexp(amax)[1] - 1 + 127, 0) - down, 1)
    scale = np.exp2(byte - 127.0)
    codes = (blocks / scale).astype(np.float32).astype(dtype).astype(np.float64)
    return np.moveaxis((codes * scale).reshape(v.shape), -1, axis)


WIDE = False


def mx_kscale(k):
    if not WIDE:
        return np.ones(k)
    levels = np.array([10, -10, 5, -5, 0])
    a = np.random.permutation(np.resize(levels, k // 512 * 4)).reshape(k // 512, 4)
    idx = np.arange(k)
    return np.exp2(a[idx // 512, idx % 128 // 32])


BF16 = ml_dtypes.bfloat16


def bf(x):
    return np.asarray(x, np.float32).astype(BF16)


def f64(x):
    return np.asarray(x).astype(np.float64)


E, CAP, D_IN, D_OUT, B, L = 4, 256, 512, 1024, 4, 1024
S = B * L


def setup_inputs():
    s = mx_kscale(D_IN)
    return {"inputs": bf(np.random.standard_normal((E * CAP, D_IN)) * s),
            "combine_weights": bf(np.random.uniform(0.0, 1.0, (S, E, CAP)) * 2.0 / np.sqrt(E * CAP)),
            "weight": bf(np.random.standard_normal((E, D_IN, D_OUT)) / np.sqrt(D_IN) / s[None, :, None]),
            "bias": bf(np.random.standard_normal((E, 1, D_OUT)) * 0.1)}


def reference(inputs, combine_weights, weight, bias):
    x = f64(inputs).reshape(E, CAP, D_IN)
    expert_out = (mxq(x, 2, "e4m3") @ mxq(f64(weight), 1, "e4m3")) + f64(bias)
    expert_out = expert_out.reshape(E, 1, CAP, D_OUT).transpose(1, 0, 2, 3)
    flat = expert_out.reshape(E * CAP, D_OUT)
    cw = f64(combine_weights).reshape(S, E * CAP)
    output = mxq(cw, 1, "e4m3") @ mxq(flat, 0, "e4m3")
    return output.reshape(B, L, D_OUT)

@@ -1,0 +1,259 @@
+from contextlib import ExitStack
+
+import concourse.bass as bass
+import concourse.mybir as mybir
+import concourse.tile as tile
+from concourse.masks import make_identity
+
+F32 = mybir.dt.float32
+BF16 = mybir.dt.bfloat16
+U32 = mybir.dt.uint32
+U8 = mybir.dt.uint8
+FP8X4 = mybir.dt.float8_e4m3fn_x4
+ADD = mybir.AluOpType.add
+
+P = 128
+E = 4
+D_IN = 512
+D_OUT = 1024
+S = 4096
+NSUP = 8
+FLOPS = 2 * 1024 * 512 * 1024 + 2 * 4096 * 1024 * 1024
+
+K_EARLY = 2
+
+
+def tile_expertparallelbehindblock_t_kernel(tc, x_in, cw_in, w_in, b_in, out):
+    nc = tc.nc
+    with ExitStack() as ctx:
+        keep = ctx.enter_context(tc.tile_pool(name="keep", bufs=1))
+        rot = ctx.enter_context(tc.tile_pool(name="rot", bufs=1))
+        psum = ctx.enter_context(tc.psum_pool(name="psum", bufs=4))
+
+        cw_rows = cw_in.rearrange("(c p j) e k -> c p j (e k)", p=P, j=4)
+        out_rows = out.rearrange("b (h p j) d -> (b h) p j d", p=P, j=4)
+
+        ident = keep.tile([P, P], F32)
+        ones = keep.tile([P, P], BF16)
+        bias_bc = keep.tile([P, E, D_OUT], BF16)
+        xq = keep.tile([P, 1024], U32, align_bytes=64)
+        xs = keep.tile([P, 1024], U8, align_bytes=64)
+        wq = keep.tile([P, E, D_OUT], U32, align_bytes=64)
+        ws = keep.tile([P, E, D_OUT], U8, align_bytes=64)
+        fg = keep.tile([P, 2, D_OUT, 4], BF16, align_bytes=64)
+        fq = keep.tile([P, 2, D_OUT], U32, align_bytes=64)
+        fs = keep.tile([P, 2, D_OUT], U8, align_bytes=64)
+        cwq = keep.tile([P, NSUP, 1024], U32, align_bytes=64)
+        cws = keep.tile([P, NSUP, 1024], U8, align_bytes=64)
+
+        brow = rot.tile([P, E * D_OUT], BF16, tag="grp", bufs=3, align_bytes=64)
+        nc.vector.memset(brow[:], 0.0)
+        nc.vector.memset(ones[:], 1.0)
+        make_identity(nc, ident[:])
+        nc.sync.dma_start(out=brow[0:1, :], in_=b_in.rearrange("e o d -> o (e d)"))
+
+        x_sb = rot.tile([P, 8, D_IN], BF16, tag="big", bufs=7)
+        nc.sync.dma_start(
+            out=x_sb[:].rearrange("p (a e) k -> p a e k", e=2),
+            in_=x_in.rearrange("(a p e) k -> p a e k", a=E, e=2),
+        )
+        w_sb = []
+        for a in range(E):
+            w_t = rot.tile([P, 4, D_OUT], BF16, tag="big", bufs=7, name="w_sb%d" % a)
+            nc.sync.dma_start(
+                out=w_t[:].rearrange("p (u e) d -> p u e d", e=2),
+                in_=w_in[a].rearrange("(u q e) d -> q u e d", u=2, e=2),
+            )
+            w_sb.append(w_t)
+
+        cw_sb = {}
+
+        def load_cw(c):
+            t = rot.tile([P, 4, 1024], BF16, tag="cw", bufs=4, name="cw_sb%d" % c)
+            nc.sync.dma_start(out=t[:], in_=cw_rows[c])
+            cw_sb[c] = t
+
+        for c in range(4):
+            load_cw(c)
+
+        def copy_on(eng, dst, src):
+            if eng == "v":
+                nc.vector.tensor_copy(out=dst, in_=src)
+            else:
+                nc.scalar.copy(out=dst, in_=src)
+
+        for a in range(E):
+            bp = psum.tile([P, D_OUT], BF16, tag="acc")
+            for h in range(2):
+                nc.tensor.matmul(
+                    bp[:, h * 512 : (h + 1) * 512],
+                    lhsT=ones[:],
+                    rhs=brow[:, a * D_OUT + h * 512 : a * D_OUT + (h + 1) * 512],
+                    start=True,
+                    stop=True,
+                )
+            nc.scalar.copy(out=bias_bc[:, a, :], in_=bp[:])
+
+        xg = rot.tile([P, 4096], BF16, tag="grp", bufs=3, align_bytes=64)
+        x_w = x_sb[:].bitcast(F32)
+        xg_w = xg[:].bitcast(F32).rearrange("p (i s u) -> p i s u", i=8, u=2)
+        for i in range(4):
+            xt = psum.tile([P, 2, 2, P], F32, tag="tr")
+            for i2 in range(2):
+                for u in range(2):
+                    nc.tensor.transpose(xt[:, i2, u, :], x_w[:, 2 * i + i2, u * P : (u + 1) * P], ident[:])
+            copy_on("s" if i % 2 == 0 else "v", xg_w[:, 2 * i : 2 * i + 2, :, :], xt[:].rearrange("p i u s -> p i s u"))
+        for h in range(2):
+            nc.vector.quantize_mx(
+                out=xq[:, h * 512 : (h + 1) * 512].bitcast(FP8X4),
+                scales=xs[:, h * 512 : (h + 1) * 512],
+                in_=xg[:, h * 2048 : (h + 1) * 2048],
+            )
+
+        wg = {}
+
+        def regroup_w(a, n, eng):
+            t = rot.tile([P, 2048], BF16, tag="wg", bufs=4, align_bytes=64, name="wg%d%d" % (a, n))
+            copy_on(
+                eng,
+                t[:].rearrange("p (c i t) -> p c t i", i=4, t=4),
+                w_sb[a][:, :, n * 512 : (n + 1) * 512].rearrange("p t (c i) -> p c t i", i=4),
+            )
+            wg[(a, n)] = t
+
+        def quant_w(a, n):
+            cols = slice(n * 512, (n + 1) * 512)
+            nc.vector.quantize_mx(out=wq[:, a, cols].bitcast(FP8X4), scales=ws[:, a, cols], in_=wg[(a, n)][:])
+
+        def stage1(g, n):
+            for dq in range(4 * n, 4 * n + 4):
+                cols = slice(dq * P, (dq + 1) * P)
+                fp = psum.tile([P, 2, 2, P], F32, tag="acc")
+                for u in range(2):
+                    a = 2 * g + u
+                    for e in range(2):
+                        xc = slice((2 * a + e) * P, (2 * a + e + 1) * P)
+                        nc.tensor.matmul_mx(
+                            out=fp[:, u, e, :],
+                            lhsT=xq[:, xc].bitcast(FP8X4),
+                            lhsT_scale=xs[:, xc],
+                            rhs=wq[:, a, cols].bitcast(FP8X4),
+                            rhs_scale=ws[:, a, cols],
+                            start=True,
+                            stop=True,
+                        )
+                nc.vector.tensor_tensor(
+                    out=fg[:, g, cols, :].rearrange("p d (u e) -> p d u e", e=2),
+                    in0=fp[:].rearrange("p u e d -> p d u e"),
+                    in1=bias_bc[:, 2 * g : 2 * g + 2, cols].rearrange("p u d -> p d u").unsqueeze(3).to_broadcast([P, P, 2, 2]),
+                    op=ADD,
+                )
+
+        def quant_f(g, n):
+            cols = slice(n * 512, (n + 1) * 512)
+            nc.vector.quantize_mx(
+                out=fq[:, g, cols].bitcast(FP8X4),
+                scales=fs[:, g, cols],
+                in_=fg[:, g, cols, :].rearrange("p d t -> p (d t)"),
+            )
+
+        def prep_cw(c, engs):
+            cwg = rot.tile([P, 4096], BF16, tag="grp", bufs=3, align_bytes=64, name="cwg%d" % c)
+            cw_w = cw_sb[c][:].bitcast(F32)
+            cwg_w = cwg[:].bitcast(F32).rearrange("p (j g s u) -> p j g s u", j=4, g=2, u=2)
+            cts = []
+            for j in range(4):
+                ct = psum.tile([P, 4, P], F32, tag="tr", name="ct%d_%d" % (c, j))
+                for a in range(4):
+                    nc.tensor.transpose(ct[:, a, :], cw_w[:, j, a * P : (a + 1) * P], ident[:])
+                cts.append(ct)
+            for j in range(4):
+                copy_on(engs[j], cwg_w[:, j], cts[j][:].rearrange("p (g u) s -> p g s u", u=2))
+            return cwg
+
+        def quant_cw(c, cwg, h):
+            nc.vector.quantize_mx(
+                out=cwq[:, c, h * 512 : (h + 1) * 512].bitcast(FP8X4),
+                scales=cws[:, c, h * 512 : (h + 1) * 512],
+                in_=cwg[:, h * 2048 : (h + 1) * 2048],
+            )
+
+        o_sb = {}
+
+        def mm(c, j, n, eng):
+            if (c, j // 2) not in o_sb:
+                o_sb[(c, j // 2)] = rot.tile([P, 2, D_OUT], F32, tag="big", bufs=7, name="o_sb%d_%d" % (c, j // 2))
+            acc = psum.tile([P, 512], F32, tag="acc", name="acc%d_%d_%d" % (c, j, n))
+            for g in range(2):
+                sc = slice((2 * j + g) * P, (2 * j + g + 1) * P)
+                nc.tensor.matmul_mx(
+                    out=acc[:],
+                    lhsT=cwq[:, c, sc].bitcast(FP8X4),
+                    lhsT_scale=cws[:, c, sc],
+                    rhs=fq[:, g, n * 512 : (n + 1) * 512].bitcast(FP8X4),
+                    rhs_scale=fs[:, g, n * 512 : (n + 1) * 512],
+                    start=(g == 0),
+                    stop=(g == 1),
+                )
+            copy_on(eng, o_sb[(c, j // 2)][:, j % 2, n * 512 : (n + 1) * 512], acc[:])
+
+        def store(c, h):
+            nc.sync.dma_start(out=out_rows[c][:, 2 * h : 2 * h + 2, :], in_=o_sb[(c, h)][:])
+
+        regroup_w(0, 0, "s")
+        regroup_w(1, 0, "s")
+        quant_w(0, 0)
+        quant_w(1, 0)
+        stage1(0, 0)
+        regroup_w(2, 0, "s")
+        regroup_w(3, 0, "v")
+        quant_w(2, 0)
+        quant_f(0, 0)
+        quant_w(3, 0)
+        stage1(1, 0)
+        quant_f(1, 0)
+
+        for c in range(K_EARLY):
+            g_t = prep_cw(c, "ssss")
+            quant_cw(c, g_t, 0)
+            quant_cw(c, g_t, 1)
+            load_cw(c + 4)
+        for c in range(K_EARLY):
+            for j in range(4):
+                mm(c, j, 0, "v" if j % 2 == 0 else "s")
+
+        regroup_w(0, 1, "s")
+        regroup_w(1, 1, "s")
+        quant_w(0, 1)
+        quant_w(1, 1)
+        stage1(0, 1)
+        regroup_w(2, 1, "s")
+        regroup_w(3, 1, "s")
+        quant_w(2, 1)
+        quant_f(0, 1)
+        quant_w(3, 1)
+        stage1(1, 1)
+        quant_f(1, 1)
+
+        g_next = prep_cw(K_EARLY, "svss")
+        load_cw(K_EARLY + 4)
+        for c in range(K_EARLY):
+            for j in range(4):
+                mm(c, j, 1, "v" if j % 2 == 0 else "s")
+                if j % 2 == 1:
+                    store(c, j // 2)
+        quant_cw(K_EARLY, g_next, 0)
+        quant_cw(K_EARLY, g_next, 1)
+
+        for c in range(K_EARLY, NSUP):
+            if c + 1 < NSUP:
+                g_next = prep_cw(c + 1, "svss")
+                if c + 5 < NSUP:
+                    load_cw(c + 5)
+            for j in range(4):
+                mm(c, j, 0, "v")
+                mm(c, j, 1, "s")
+                if j % 2 == 1:
+                    store(c, j // 2)
+                if c + 1 < NSUP and j in (1, 2):
+                    quant_cw(c + 1, g_next, j - 1)

@@ -1,8 +1,6 @@
 from contextlib import ExitStack
 
-import concourse.bass as bass
 import concourse.mybir as mybir
-import concourse.tile as tile
 from concourse.masks import make_identity
 
 F32 = mybir.dt.float32
@@ -16,11 +14,64 @@ P = 128
 E = 4
 D_IN = 512
 D_OUT = 1024
-S = 4096
-NSUP = 8
 FLOPS = 2 * 1024 * 512 * 1024 + 2 * 4096 * 1024 * 1024
+KE = 4
+PINNED = True
 
-K_EARLY = 2
+ORDER = (
+    ("ms",), ("id",), ("lb",), ("lx",), ("lw", 0), ("lw", 1),
+    ("lw", 2), ("lw", 3), ("lc", 0), ("lc", 1), ("lc", 2), ("bm", 0),
+    ("bm", 1), ("bc", 0), ("bm", 2), ("bc", 1), ("bm", 3), ("bc", 2),
+    ("lc", 3), ("xT", 0), ("bc", 3), ("xT", 1), ("xc", 0, "s"), ("xT", 2),
+    ("xT", 3), ("xc", 1, "s"), ("xc", 2, "s"), ("lc", 4), ("R", 0, 0, "v"), ("xc", 3, "s"),
+    ("qx", 0), ("qx", 1), ("lc", 5), ("R", 1, 0, "s"), ("qW", 0, 0), ("R", 0, 1, "v"),
+    ("R", 1, 1, "v"), ("lc", 6), ("R", 2, 0, "s"), ("qW", 1, 0), ("qW", 0, 1), ("S1", 0, 0, 0),
+    ("qW", 1, 1), ("S1", 0, 0, 1), ("R", 3, 0, "s"), ("S1", 0, 0, 2), ("B", 0, 0, 0), ("S1", 0, 0, 3),
+    ("B", 0, 0, 1), ("B", 0, 0, 2), ("B", 0, 0, 3), ("lc", 7), ("T", 0, 0), ("T", 0, 1),
+    ("qW", 2, 0), ("Tc", 0, 0, "s"), ("T", 0, 2), ("qF", 0, 0), ("T", 0, 3), ("Tc", 0, 1, "s"),
+    ("qW", 3, 0), ("Tc", 0, 2, "s"), ("R", 3, 1, "v"), ("T", 1, 0), ("Tc", 0, 3, "s"), ("T", 1, 1),
+    ("Tc", 1, 0, "s"), ("S1", 1, 0, 0), ("S1", 1, 0, 1), ("qC", 0, 0), ("Tc", 1, 1, "s"), ("S1", 1, 0, 2),
+    ("B", 1, 0, 0), ("S1", 1, 0, 3), ("T", 1, 2), ("B", 1, 0, 1), ("T", 1, 3), ("Tc", 1, 2, "s"),
+    ("T", 2, 0), ("B", 1, 0, 2), ("T", 2, 1), ("Tc", 1, 3, "s"), ("T", 2, 2), ("B", 1, 0, 3),
+    ("Tc", 2, 0, "s"), ("T", 2, 3), ("qF", 1, 0), ("Tc", 2, 1, "s"), ("T", 3, 0), ("qC", 0, 1),
+    ("Tc", 2, 2, "s"), ("T", 3, 1), ("qC", 1, 0), ("Tc", 2, 3, "s"), ("T", 3, 2), ("MM", 0, 0, 0),
+    ("Tc", 3, 0, "s"), ("qC", 1, 1), ("Tc", 3, 1, "s"), ("MM", 0, 1, 0), ("R", 2, 1, "v"), ("O", 0, 0, 0, "s"),
+    ("MM", 0, 2, 0), ("O", 0, 1, 0, "s"), ("MM", 0, 3, 0), ("qC", 2, 0), ("O", 0, 2, 0, "s"), ("S1", 0, 1, 0),
+    ("qC", 2, 1), ("S1", 0, 1, 1), ("O", 0, 3, 0, "s"), ("MM", 1, 0, 0), ("B", 0, 1, 0), ("Tc", 3, 2, "s"),
+    ("S1", 0, 1, 2), ("st", 0, 0), ("B", 0, 1, 1), ("S1", 0, 1, 3), ("O", 1, 0, 0, "s"), ("MM", 1, 1, 0),
+    ("B", 0, 1, 2), ("MM", 1, 2, 0), ("O", 1, 1, 0, "s"), ("B", 0, 1, 3), ("MM", 1, 3, 0), ("O", 1, 2, 0, "s"),
+    ("qW", 2, 1), ("T", 3, 3), ("O", 1, 3, 0, "s"), ("qF", 0, 1), ("MM", 2, 0, 0), ("Tc", 3, 3, "s"),
+    ("st", 1, 0), ("qW", 3, 1), ("MM", 2, 1, 0), ("O", 2, 0, 0, "s"), ("qC", 3, 0), ("MM", 2, 2, 0),
+    ("O", 2, 1, 0, "s"), ("qC", 3, 1), ("MM", 2, 3, 0), ("O", 2, 2, 0, "s"), ("S1", 1, 1, 0), ("O", 2, 3, 0, "s"),
+    ("S1", 1, 1, 1), ("B", 1, 1, 0), ("S1", 1, 1, 2), ("st", 2, 0), ("S1", 1, 1, 3), ("B", 1, 1, 1),
+    ("T", 4, 0), ("T", 4, 1), ("B", 1, 1, 2), ("Tc", 4, 0, "s"), ("T", 4, 2), ("T", 4, 3),
+    ("B", 1, 1, 3), ("Tc", 4, 1, "s"), ("MM", 3, 0, 0), ("Tc", 4, 2, "s"), ("qF", 1, 1), ("MM", 3, 1, 0),
+    ("Tc", 4, 3, "s"), ("MM", 3, 2, 0), ("O", 3, 0, 0, "s"), ("qC", 4, 0), ("MM", 3, 3, 0), ("O", 3, 1, 0, "s"),
+    ("qC", 4, 1), ("T", 5, 0), ("O", 3, 2, 0, "s"), ("T", 5, 1), ("O", 3, 3, 0, "s"), ("T", 5, 2),
+    ("T", 5, 3), ("Tc", 5, 0, "s"), ("MM", 0, 0, 1), ("st", 3, 0), ("Tc", 5, 1, "s"), ("MM", 0, 1, 1),
+    ("O", 0, 0, 1, "v"), ("Tc", 5, 2, "s"), ("MM", 0, 2, 1), ("Tc", 5, 3, "s"), ("MM", 0, 3, 1), ("O", 0, 2, 1, "v"),
+    ("O", 0, 1, 1, "s"), ("MM", 1, 0, 1), ("qC", 5, 0), ("O", 0, 3, 1, "s"), ("MM", 1, 1, 1), ("O", 1, 0, 1, "v"),
+    ("st", 0, 1), ("MM", 1, 2, 1), ("O", 1, 1, 1, "s"), ("qC", 5, 1), ("MM", 1, 3, 1), ("O", 1, 2, 1, "v"),
+    ("MM", 2, 0, 1), ("O", 1, 3, 1, "s"), ("MM", 2, 1, 1), ("O", 2, 0, 1, "v"), ("st", 1, 1), ("MM", 2, 2, 1),
+    ("O", 2, 1, 1, "s"), ("MM", 2, 3, 1), ("O", 2, 2, 1, "v"), ("MM", 3, 0, 1), ("O", 2, 3, 1, "s"), ("MM", 3, 1, 1),
+    ("O", 3, 0, 1, "v"), ("st", 2, 1), ("MM", 3, 2, 1), ("O", 3, 1, 1, "s"), ("MM", 3, 3, 1), ("O", 3, 2, 1, "v"),
+    ("MM", 4, 0, 0), ("O", 3, 3, 1, "s"), ("MM", 4, 0, 1), ("O", 4, 0, 0, "v"), ("st", 3, 1), ("MM", 4, 1, 0),
+    ("O", 4, 0, 1, "s"), ("MM", 4, 1, 1), ("O", 4, 1, 0, "v"), ("MM", 4, 2, 0), ("O", 4, 1, 1, "s"), ("MM", 4, 2, 1),
+    ("O", 4, 2, 0, "v"), ("st", 4, 0), ("MM", 4, 3, 0), ("O", 4, 2, 1, "s"), ("MM", 4, 3, 1), ("O", 4, 3, 0, "v"),
+    ("T", 6, 0), ("O", 4, 3, 1, "s"), ("T", 6, 1), ("Tc", 6, 0, "s"), ("T", 6, 2), ("st", 4, 1),
+    ("Tc", 6, 1, "v"), ("T", 6, 3), ("Tc", 6, 2, "s"), ("MM", 5, 0, 0), ("Tc", 6, 3, "s"), ("MM", 5, 0, 1),
+    ("O", 5, 0, 0, "v"), ("MM", 5, 1, 0), ("O", 5, 0, 1, "s"), ("qC", 6, 0), ("MM", 5, 1, 1), ("O", 5, 1, 0, "v"),
+    ("MM", 5, 2, 0), ("O", 5, 1, 1, "s"), ("qC", 6, 1), ("MM", 5, 2, 1), ("O", 5, 2, 0, "v"), ("st", 5, 0),
+    ("MM", 5, 3, 0), ("O", 5, 2, 1, "s"), ("MM", 5, 3, 1), ("O", 5, 3, 0, "v"), ("T", 7, 0), ("O", 5, 3, 1, "s"),
+    ("T", 7, 1), ("Tc", 7, 0, "s"), ("T", 7, 2), ("st", 5, 1), ("Tc", 7, 1, "v"), ("T", 7, 3),
+    ("Tc", 7, 2, "s"), ("MM", 6, 0, 0), ("Tc", 7, 3, "s"), ("MM", 6, 0, 1), ("O", 6, 0, 0, "v"), ("MM", 6, 1, 0),
+    ("O", 6, 0, 1, "s"), ("qC", 7, 0), ("MM", 6, 1, 1), ("O", 6, 1, 0, "v"), ("MM", 6, 2, 0), ("O", 6, 1, 1, "s"),
+    ("qC", 7, 1), ("MM", 6, 2, 1), ("O", 6, 2, 0, "v"), ("st", 6, 0), ("MM", 6, 3, 0), ("O", 6, 2, 1, "s"),
+    ("MM", 6, 3, 1), ("O", 6, 3, 0, "v"), ("MM", 7, 0, 0), ("O", 6, 3, 1, "s"), ("MM", 7, 0, 1), ("O", 7, 0, 0, "v"),
+    ("st", 6, 1), ("MM", 7, 1, 0), ("O", 7, 0, 1, "s"), ("MM", 7, 1, 1), ("O", 7, 1, 0, "v"), ("MM", 7, 2, 0),
+    ("O", 7, 1, 1, "s"), ("MM", 7, 2, 1), ("O", 7, 2, 0, "v"), ("st", 7, 0), ("MM", 7, 3, 0), ("O", 7, 2, 1, "s"),
+    ("MM", 7, 3, 1), ("O", 7, 3, 0, "v"), ("O", 7, 3, 1, "s"), ("st", 7, 1),
+)
 
 
 def tile_expertparallelbehindblock_t_kernel(tc, x_in, cw_in, w_in, b_in, out):
@@ -29,6 +80,8 @@ def tile_expertparallelbehindblock_t_kernel(tc, x_in, cw_in, w_in, b_in, out):
         keep = ctx.enter_context(tc.tile_pool(name="keep", bufs=1))
         rot = ctx.enter_context(tc.tile_pool(name="rot", bufs=1))
         psum = ctx.enter_context(tc.psum_pool(name="psum", bufs=4))
+        if PINNED:
+            ctx.enter_context(tc.manual_schedule())
 
         cw_rows = cw_in.rearrange("(c p j) e k -> c p j (e k)", p=P, j=4)
         out_rows = out.rearrange("b (h p j) d -> (b h) p j d", p=P, j=4)
@@ -40,41 +93,14 @@ def tile_expertparallelbehindblock_t_kernel(tc, x_in, cw_in, w_in, b_in, out):
         xs = keep.tile([P, 1024], U8, align_bytes=64)
         wq = keep.tile([P, E, D_OUT], U32, align_bytes=64)
         ws = keep.tile([P, E, D_OUT], U8, align_bytes=64)
-        fg = keep.tile([P, 2, D_OUT, 4], BF16, align_bytes=64)
         fq = keep.tile([P, 2, D_OUT], U32, align_bytes=64)
         fs = keep.tile([P, 2, D_OUT], U8, align_bytes=64)
-        cwq = keep.tile([P, NSUP, 1024], U32, align_bytes=64)
-        cws = keep.tile([P, NSUP, 1024], U8, align_bytes=64)
 
-        brow = rot.tile([P, E * D_OUT], BF16, tag="grp", bufs=3, align_bytes=64)
-        nc.vector.memset(brow[:], 0.0)
-        nc.vector.memset(ones[:], 1.0)
-        make_identity(nc, ident[:])
-        nc.sync.dma_start(out=brow[0:1, :], in_=b_in.rearrange("e o d -> o (e d)"))
+        t = {}
 
-        x_sb = rot.tile([P, 8, D_IN], BF16, tag="big", bufs=7)
-        nc.sync.dma_start(
-            out=x_sb[:].rearrange("p (a e) k -> p a e k", e=2),
-            in_=x_in.rearrange("(a p e) k -> p a e k", a=E, e=2),
-        )
-        w_sb = []
-        for a in range(E):
-            w_t = rot.tile([P, 4, D_OUT], BF16, tag="big", bufs=7, name="w_sb%d" % a)
-            nc.sync.dma_start(
-                out=w_t[:].rearrange("p (u e) d -> p u e d", e=2),
-                in_=w_in[a].rearrange("(u q e) d -> q u e d", u=2, e=2),
-            )
-            w_sb.append(w_t)
-
-        cw_sb = {}
-
-        def load_cw(c):
-            t = rot.tile([P, 4, 1024], BF16, tag="cw", bufs=4, name="cw_sb%d" % c)
-            nc.sync.dma_start(out=t[:], in_=cw_rows[c])
-            cw_sb[c] = t
-
-        for c in range(4):
-            load_cw(c)
+        def big(name, shape, dtype):
+            t[name] = rot.tile(shape, dtype, tag="big", bufs=7, align_bytes=64, name=name)
+            return t[name]
 
         def copy_on(eng, dst, src):
             if eng == "v":
@@ -82,178 +108,185 @@ def tile_expertparallelbehindblock_t_kernel(tc, x_in, cw_in, w_in, b_in, out):
             else:
                 nc.scalar.copy(out=dst, in_=src)
 
-        for a in range(E):
-            bp = psum.tile([P, D_OUT], BF16, tag="acc")
+        def op_ms():
+            big("brow", [P, E * D_OUT], BF16)
+            nc.vector.memset(t["brow"][:], 0.0)
+            nc.vector.memset(ones[:], 1.0)
+
+        def op_id():
+            make_identity(nc, ident[:])
+
+        def op_lb():
+            nc.sync.dma_start(out=t["brow"][0:1, :], in_=b_in.rearrange("e o d -> o (e d)"))
+
+        def op_lx():
+            big("x", [P, 8, D_IN], BF16)
+            nc.sync.dma_start(
+                out=t["x"][:].rearrange("p (a e) k -> p a e k", e=2),
+                in_=x_in.rearrange("(a p e) k -> p a e k", a=E, e=2),
+            )
+
+        def op_lw(a):
+            w_t = big("w%d" % a, [P, 4, D_OUT], BF16)
+            nc.sync.dma_start(
+                out=w_t[:].rearrange("p (u e) d -> p u e d", e=2),
+                in_=w_in[a].rearrange("(u q e) d -> q u e d", u=2, e=2),
+            )
+
+        def op_lc(c):
+            t["cw%d" % c] = rot.tile([P, 4, 1024], BF16, tag="cw", bufs=7, name="cw%d" % c)
+            nc.sync.dma_start(out=t["cw%d" % c][:], in_=cw_rows[c])
+
+        def op_bm(a):
+            bp = psum.tile([P, D_OUT], BF16, tag="acc", name="bp%d" % a)
+            t["bp%d" % a] = bp
             for h in range(2):
                 nc.tensor.matmul(
                     bp[:, h * 512 : (h + 1) * 512],
                     lhsT=ones[:],
-                    rhs=brow[:, a * D_OUT + h * 512 : a * D_OUT + (h + 1) * 512],
+                    rhs=t["brow"][:, a * D_OUT + h * 512 : a * D_OUT + (h + 1) * 512],
                     start=True,
                     stop=True,
                 )
-            nc.scalar.copy(out=bias_bc[:, a, :], in_=bp[:])
 
-        xg = rot.tile([P, 4096], BF16, tag="grp", bufs=3, align_bytes=64)
-        x_w = x_sb[:].bitcast(F32)
-        xg_w = xg[:].bitcast(F32).rearrange("p (i s u) -> p i s u", i=8, u=2)
-        for i in range(4):
-            xt = psum.tile([P, 2, 2, P], F32, tag="tr")
+        def op_bc(a):
+            nc.scalar.copy(out=bias_bc[:, a, :], in_=t["bp%d" % a][:])
+
+        def op_xT(i):
+            xt = psum.tile([P, 2, 2, P], F32, tag="tr", name="xt%d" % i)
+            t["xt%d" % i] = xt
+            x_w = t["x"][:].bitcast(F32)
             for i2 in range(2):
                 for u in range(2):
                     nc.tensor.transpose(xt[:, i2, u, :], x_w[:, 2 * i + i2, u * P : (u + 1) * P], ident[:])
-            copy_on("s" if i % 2 == 0 else "v", xg_w[:, 2 * i : 2 * i + 2, :, :], xt[:].rearrange("p i u s -> p i s u"))
-        for h in range(2):
+
+        def op_xc(i, eng):
+            if "xg" not in t:
+                big("xg", [P, 4096], BF16)
+            xg_w = t["xg"][:].bitcast(F32).rearrange("p (i s u) -> p i s u", i=8, u=2)
+            copy_on(eng, xg_w[:, 2 * i : 2 * i + 2, :, :], t["xt%d" % i][:].rearrange("p i u s -> p i s u"))
+
+        def op_qx(h):
             nc.vector.quantize_mx(
                 out=xq[:, h * 512 : (h + 1) * 512].bitcast(FP8X4),
                 scales=xs[:, h * 512 : (h + 1) * 512],
-                in_=xg[:, h * 2048 : (h + 1) * 2048],
+                in_=t["xg"][:, h * 2048 : (h + 1) * 2048],
             )
 
-        wg = {}
-
-        def regroup_w(a, n, eng):
-            t = rot.tile([P, 2048], BF16, tag="wg", bufs=4, align_bytes=64, name="wg%d%d" % (a, n))
+        def op_R(a, n, eng):
+            g_t = rot.tile([P, 2048], BF16, tag="wg", bufs=5, align_bytes=64, name="wg%d%d" % (a, n))
+            t["wg%d%d" % (a, n)] = g_t
             copy_on(
                 eng,
-                t[:].rearrange("p (c i t) -> p c t i", i=4, t=4),
-                w_sb[a][:, :, n * 512 : (n + 1) * 512].rearrange("p t (c i) -> p c t i", i=4),
+                g_t[:].rearrange("p (c i t) -> p c t i", i=4, t=4),
+                t["w%d" % a][:, :, n * 512 : (n + 1) * 512].rearrange("p t (c i) -> p c t i", i=4),
             )
-            wg[(a, n)] = t
 
-        def quant_w(a, n):
+        def op_qW(a, n):
             cols = slice(n * 512, (n + 1) * 512)
-            nc.vector.quantize_mx(out=wq[:, a, cols].bitcast(FP8X4), scales=ws[:, a, cols], in_=wg[(a, n)][:])
+            nc.vector.quantize_mx(out=wq[:, a, cols].bitcast(FP8X4), scales=ws[:, a, cols], in_=t["wg%d%d" % (a, n)][:])
 
-        def stage1(g, n):
-            for dq in range(4 * n, 4 * n + 4):
-                cols = slice(dq * P, (dq + 1) * P)
-                fp = psum.tile([P, 2, 2, P], F32, tag="acc")
-                for u in range(2):
-                    a = 2 * g + u
-                    for e in range(2):
-                        xc = slice((2 * a + e) * P, (2 * a + e + 1) * P)
-                        nc.tensor.matmul_mx(
-                            out=fp[:, u, e, :],
-                            lhsT=xq[:, xc].bitcast(FP8X4),
-                            lhsT_scale=xs[:, xc],
-                            rhs=wq[:, a, cols].bitcast(FP8X4),
-                            rhs_scale=ws[:, a, cols],
-                            start=True,
-                            stop=True,
-                        )
-                nc.vector.tensor_tensor(
-                    out=fg[:, g, cols, :].rearrange("p d (u e) -> p d u e", e=2),
-                    in0=fp[:].rearrange("p u e d -> p d u e"),
-                    in1=bias_bc[:, 2 * g : 2 * g + 2, cols].rearrange("p u d -> p d u").unsqueeze(3).to_broadcast([P, P, 2, 2]),
-                    op=ADD,
-                )
+        def op_S1(g, n, d):
+            cols = slice((4 * n + d) * P, (4 * n + d + 1) * P)
+            fp = psum.tile([P, 2, 2, P], F32, tag="acc", name="fp%d%d%d" % (g, n, d))
+            t["fp%d%d%d" % (g, n, d)] = fp
+            for u in range(2):
+                a = 2 * g + u
+                for e in range(2):
+                    xc = slice((2 * a + e) * P, (2 * a + e + 1) * P)
+                    nc.tensor.matmul_mx(
+                        out=fp[:, u, e, :],
+                        lhsT=xq[:, xc].bitcast(FP8X4),
+                        lhsT_scale=xs[:, xc],
+                        rhs=wq[:, a, cols].bitcast(FP8X4),
+                        rhs_scale=ws[:, a, cols],
+                        start=True,
+                        stop=True,
+                    )
 
-        def quant_f(g, n):
+        def op_B(g, n, d):
+            key = "fg%d%d" % (g, n)
+            if key not in t:
+                t[key] = rot.tile([P, 512, 4], BF16, tag="wg", bufs=5, align_bytes=64, name=key)
+            cols = slice((4 * n + d) * P, (4 * n + d + 1) * P)
+            nc.vector.tensor_tensor(
+                out=t[key][:, d * P : (d + 1) * P, :].rearrange("p d (u e) -> p d u e", e=2),
+                in0=t["fp%d%d%d" % (g, n, d)][:].rearrange("p u e d -> p d u e"),
+                in1=bias_bc[:, 2 * g : 2 * g + 2, cols].rearrange("p u d -> p d u").unsqueeze(3).to_broadcast([P, P, 2, 2]),
+                op=ADD,
+            )
+
+        def op_qF(g, n):
             cols = slice(n * 512, (n + 1) * 512)
             nc.vector.quantize_mx(
                 out=fq[:, g, cols].bitcast(FP8X4),
                 scales=fs[:, g, cols],
-                in_=fg[:, g, cols, :].rearrange("p d t -> p (d t)"),
+                in_=t["fg%d%d" % (g, n)][:].rearrange("p d t -> p (d t)"),
             )
 
-        def prep_cw(c, engs):
-            cwg = rot.tile([P, 4096], BF16, tag="grp", bufs=3, align_bytes=64, name="cwg%d" % c)
-            cw_w = cw_sb[c][:].bitcast(F32)
-            cwg_w = cwg[:].bitcast(F32).rearrange("p (j g s u) -> p j g s u", j=4, g=2, u=2)
-            cts = []
-            for j in range(4):
-                ct = psum.tile([P, 4, P], F32, tag="tr", name="ct%d_%d" % (c, j))
-                for a in range(4):
-                    nc.tensor.transpose(ct[:, a, :], cw_w[:, j, a * P : (a + 1) * P], ident[:])
-                cts.append(ct)
-            for j in range(4):
-                copy_on(engs[j], cwg_w[:, j], cts[j][:].rearrange("p (g u) s -> p g s u", u=2))
-            return cwg
+        def op_T(c, j):
+            ct = psum.tile([P, 4, P], F32, tag="tr", name="ct%d%d" % (c, j))
+            t["ct%d%d" % (c, j)] = ct
+            cw_w = t["cw%d" % c][:].bitcast(F32)
+            for a in range(4):
+                nc.tensor.transpose(ct[:, a, :], cw_w[:, j, a * P : (a + 1) * P], ident[:])
 
-        def quant_cw(c, cwg, h):
+        def op_Tc(c, j, eng):
+            key = "cwg%d" % c
+            if key not in t:
+                t[key] = rot.tile([P, 4096], BF16, tag="cwg", bufs=3, align_bytes=64, name=key)
+            cwg_w = t[key][:].bitcast(F32).rearrange("p (j g s u) -> p j g s u", j=4, g=2, u=2)
+            copy_on(eng, cwg_w[:, j], t["ct%d%d" % (c, j)][:].rearrange("p (g u) s -> p g s u", u=2))
+
+        def op_qC(c, h):
+            key = "cwq%d" % c
+            if key not in t:
+                t[key] = rot.tile([P, 1024], U32, tag="cwq", bufs=5, align_bytes=64, name=key)
+                t["cws%d" % c] = rot.tile([P, 1024], U8, tag="cws", bufs=5, align_bytes=64, name="cws%d" % c)
             nc.vector.quantize_mx(
-                out=cwq[:, c, h * 512 : (h + 1) * 512].bitcast(FP8X4),
-                scales=cws[:, c, h * 512 : (h + 1) * 512],
-                in_=cwg[:, h * 2048 : (h + 1) * 2048],
+                out=t[key][:, h * 512 : (h + 1) * 512].bitcast(FP8X4),
+                scales=t["cws%d" % c][:, h * 512 : (h + 1) * 512],
+                in_=t["cwg%d" % c][:, h * 2048 : (h + 1) * 2048],
             )
 
-        o_sb = {}
-
-        def mm(c, j, n, eng):
-            if (c, j // 2) not in o_sb:
-                o_sb[(c, j // 2)] = rot.tile([P, 2, D_OUT], F32, tag="big", bufs=7, name="o_sb%d_%d" % (c, j // 2))
-            acc = psum.tile([P, 512], F32, tag="acc", name="acc%d_%d_%d" % (c, j, n))
+        def op_MM(c, j, n):
+            acc = psum.tile([P, 512], F32, tag="acc", name="acc%d%d%d" % (c, j, n))
+            t["acc%d%d%d" % (c, j, n)] = acc
             for g in range(2):
                 sc = slice((2 * j + g) * P, (2 * j + g + 1) * P)
                 nc.tensor.matmul_mx(
                     out=acc[:],
-                    lhsT=cwq[:, c, sc].bitcast(FP8X4),
-                    lhsT_scale=cws[:, c, sc],
+                    lhsT=t["cwq%d" % c][:, sc].bitcast(FP8X4),
+                    lhsT_scale=t["cws%d" % c][:, sc],
                     rhs=fq[:, g, n * 512 : (n + 1) * 512].bitcast(FP8X4),
                     rhs_scale=fs[:, g, n * 512 : (n + 1) * 512],
                     start=(g == 0),
                     stop=(g == 1),
                 )
-            copy_on(eng, o_sb[(c, j // 2)][:, j % 2, n * 512 : (n + 1) * 512], acc[:])
 
-        def store(c, h):
-            nc.sync.dma_start(out=out_rows[c][:, 2 * h : 2 * h + 2, :], in_=o_sb[(c, h)][:])
+        def op_O(c, j, n, eng):
+            acc = t["acc%d%d%d" % (c, j, n)]
+            if c < KE:
+                key = "o%dn%d" % (c, n)
+                if key not in t:
+                    big(key, [P, 4, 512], F32)
+                copy_on(eng, t[key][:, j, :], acc[:])
+            else:
+                key = "o%dh%d" % (c, j // 2)
+                if key not in t:
+                    big(key, [P, 2, D_OUT], F32)
+                copy_on(eng, t[key][:, j % 2, n * 512 : (n + 1) * 512], acc[:])
 
-        regroup_w(0, 0, "s")
-        regroup_w(1, 0, "s")
-        quant_w(0, 0)
-        quant_w(1, 0)
-        stage1(0, 0)
-        regroup_w(2, 0, "s")
-        regroup_w(3, 0, "v")
-        quant_w(2, 0)
-        quant_f(0, 0)
-        quant_w(3, 0)
-        stage1(1, 0)
-        quant_f(1, 0)
+        def op_st(c, x):
+            if c < KE:
+                nc.sync.dma_start(out=out_rows[c][:, :, x * 512 : (x + 1) * 512], in_=t["o%dn%d" % (c, x)][:])
+            else:
+                nc.sync.dma_start(out=out_rows[c][:, 2 * x : 2 * x + 2, :], in_=t["o%dh%d" % (c, x)][:])
 
-        for c in range(K_EARLY):
-            g_t = prep_cw(c, "ssss")
-            quant_cw(c, g_t, 0)
-            quant_cw(c, g_t, 1)
-            load_cw(c + 4)
-        for c in range(K_EARLY):
-            for j in range(4):
-                mm(c, j, 0, "v" if j % 2 == 0 else "s")
-
-        regroup_w(0, 1, "s")
-        regroup_w(1, 1, "s")
-        quant_w(0, 1)
-        quant_w(1, 1)
-        stage1(0, 1)
-        regroup_w(2, 1, "s")
-        regroup_w(3, 1, "s")
-        quant_w(2, 1)
-        quant_f(0, 1)
-        quant_w(3, 1)
-        stage1(1, 1)
-        quant_f(1, 1)
-
-        g_next = prep_cw(K_EARLY, "svss")
-        load_cw(K_EARLY + 4)
-        for c in range(K_EARLY):
-            for j in range(4):
-                mm(c, j, 1, "v" if j % 2 == 0 else "s")
-                if j % 2 == 1:
-                    store(c, j // 2)
-        quant_cw(K_EARLY, g_next, 0)
-        quant_cw(K_EARLY, g_next, 1)
-
-        for c in range(K_EARLY, NSUP):
-            if c + 1 < NSUP:
-                g_next = prep_cw(c + 1, "svss")
-                if c + 5 < NSUP:
-                    load_cw(c + 5)
-            for j in range(4):
-                mm(c, j, 0, "v")
-                mm(c, j, 1, "s")
-                if j % 2 == 1:
-                    store(c, j // 2)
-                if c + 1 < NSUP and j in (1, 2):
-                    quant_cw(c + 1, g_next, j - 1)
+        ops = {
+            "ms": op_ms, "id": op_id, "lb": op_lb, "lx": op_lx, "lw": op_lw, "lc": op_lc, "bm": op_bm, "bc": op_bc,
+            "xT": op_xT, "xc": op_xc, "qx": op_qx, "R": op_R, "qW": op_qW, "S1": op_S1, "B": op_B, "qF": op_qF,
+            "T": op_T, "Tc": op_Tc, "qC": op_qC, "MM": op_MM, "O": op_O, "st": op_st,
+        }
+        for step in ORDER:
+            ops[step[0]](*step[1:])

@@ -7,6 +7,7 @@ F32 = mybir.dt.float32
 BF16 = mybir.dt.bfloat16
 U32 = mybir.dt.uint32
 U8 = mybir.dt.uint8
+I32 = mybir.dt.int32
 FP8X4 = mybir.dt.float8_e4m3fn_x4
 ADD = mybir.AluOpType.add
 
@@ -18,59 +19,62 @@ FLOPS = 2 * 1024 * 512 * 1024 + 2 * 4096 * 1024 * 1024
 KE = 4
 PINNED = True
 
+FINE = (6, 7)
+
 ORDER = (
-    ("ms",), ("id",), ("lb",), ("lx",), ("lw", 0), ("lw", 1),
-    ("lw", 2), ("lw", 3), ("lc", 0), ("lc", 1), ("lc", 2), ("bm", 0),
-    ("bm", 1), ("bc", 0), ("bm", 2), ("bc", 1), ("bm", 3), ("bc", 2),
-    ("lc", 3), ("xT", 0), ("bc", 3), ("xT", 1), ("xc", 0, "s"), ("xT", 2),
-    ("xT", 3), ("xc", 1, "s"), ("xc", 2, "s"), ("lc", 4), ("R", 0, 0, "v"), ("xc", 3, "s"),
-    ("qx", 0), ("qx", 1), ("lc", 5), ("R", 1, 0, "s"), ("qW", 0, 0), ("R", 0, 1, "v"),
-    ("R", 1, 1, "v"), ("lc", 6), ("R", 2, 0, "s"), ("qW", 1, 0), ("qW", 0, 1), ("S1", 0, 0, 0),
-    ("qW", 1, 1), ("S1", 0, 0, 1), ("R", 3, 0, "s"), ("S1", 0, 0, 2), ("B", 0, 0, 0), ("S1", 0, 0, 3),
-    ("B", 0, 0, 1), ("B", 0, 0, 2), ("B", 0, 0, 3), ("lc", 7), ("T", 0, 0), ("T", 0, 1),
-    ("qW", 2, 0), ("Tc", 0, 0, "s"), ("T", 0, 2), ("qF", 0, 0), ("T", 0, 3), ("Tc", 0, 1, "s"),
-    ("qW", 3, 0), ("Tc", 0, 2, "s"), ("R", 3, 1, "v"), ("T", 1, 0), ("Tc", 0, 3, "s"), ("T", 1, 1),
-    ("Tc", 1, 0, "s"), ("S1", 1, 0, 0), ("S1", 1, 0, 1), ("qC", 0, 0), ("Tc", 1, 1, "s"), ("S1", 1, 0, 2),
-    ("B", 1, 0, 0), ("S1", 1, 0, 3), ("T", 1, 2), ("B", 1, 0, 1), ("T", 1, 3), ("Tc", 1, 2, "s"),
-    ("T", 2, 0), ("B", 1, 0, 2), ("T", 2, 1), ("Tc", 1, 3, "s"), ("T", 2, 2), ("B", 1, 0, 3),
-    ("Tc", 2, 0, "s"), ("T", 2, 3), ("qF", 1, 0), ("Tc", 2, 1, "s"), ("T", 3, 0), ("qC", 0, 1),
-    ("Tc", 2, 2, "s"), ("T", 3, 1), ("qC", 1, 0), ("Tc", 2, 3, "s"), ("T", 3, 2), ("MM", 0, 0, 0),
-    ("Tc", 3, 0, "s"), ("qC", 1, 1), ("Tc", 3, 1, "s"), ("MM", 0, 1, 0), ("R", 2, 1, "v"), ("O", 0, 0, 0, "s"),
-    ("MM", 0, 2, 0), ("O", 0, 1, 0, "s"), ("MM", 0, 3, 0), ("qC", 2, 0), ("O", 0, 2, 0, "s"), ("S1", 0, 1, 0),
-    ("qC", 2, 1), ("S1", 0, 1, 1), ("O", 0, 3, 0, "s"), ("MM", 1, 0, 0), ("B", 0, 1, 0), ("Tc", 3, 2, "s"),
-    ("S1", 0, 1, 2), ("st", 0, 0), ("B", 0, 1, 1), ("S1", 0, 1, 3), ("O", 1, 0, 0, "s"), ("MM", 1, 1, 0),
-    ("B", 0, 1, 2), ("MM", 1, 2, 0), ("O", 1, 1, 0, "s"), ("B", 0, 1, 3), ("MM", 1, 3, 0), ("O", 1, 2, 0, "s"),
-    ("qW", 2, 1), ("T", 3, 3), ("O", 1, 3, 0, "s"), ("qF", 0, 1), ("MM", 2, 0, 0), ("Tc", 3, 3, "s"),
-    ("st", 1, 0), ("qW", 3, 1), ("MM", 2, 1, 0), ("O", 2, 0, 0, "s"), ("qC", 3, 0), ("MM", 2, 2, 0),
-    ("O", 2, 1, 0, "s"), ("qC", 3, 1), ("MM", 2, 3, 0), ("O", 2, 2, 0, "s"), ("S1", 1, 1, 0), ("O", 2, 3, 0, "s"),
-    ("S1", 1, 1, 1), ("B", 1, 1, 0), ("S1", 1, 1, 2), ("st", 2, 0), ("S1", 1, 1, 3), ("B", 1, 1, 1),
-    ("T", 4, 0), ("T", 4, 1), ("B", 1, 1, 2), ("Tc", 4, 0, "s"), ("T", 4, 2), ("T", 4, 3),
-    ("B", 1, 1, 3), ("Tc", 4, 1, "s"), ("MM", 3, 0, 0), ("Tc", 4, 2, "s"), ("qF", 1, 1), ("MM", 3, 1, 0),
-    ("Tc", 4, 3, "s"), ("MM", 3, 2, 0), ("O", 3, 0, 0, "s"), ("qC", 4, 0), ("MM", 3, 3, 0), ("O", 3, 1, 0, "s"),
-    ("qC", 4, 1), ("T", 5, 0), ("O", 3, 2, 0, "s"), ("T", 5, 1), ("O", 3, 3, 0, "s"), ("T", 5, 2),
-    ("T", 5, 3), ("Tc", 5, 0, "s"), ("MM", 0, 0, 1), ("st", 3, 0), ("Tc", 5, 1, "s"), ("MM", 0, 1, 1),
-    ("O", 0, 0, 1, "v"), ("Tc", 5, 2, "s"), ("MM", 0, 2, 1), ("Tc", 5, 3, "s"), ("MM", 0, 3, 1), ("O", 0, 2, 1, "v"),
-    ("O", 0, 1, 1, "s"), ("MM", 1, 0, 1), ("qC", 5, 0), ("O", 0, 3, 1, "s"), ("MM", 1, 1, 1), ("O", 1, 0, 1, "v"),
-    ("st", 0, 1), ("MM", 1, 2, 1), ("O", 1, 1, 1, "s"), ("qC", 5, 1), ("MM", 1, 3, 1), ("O", 1, 2, 1, "v"),
-    ("MM", 2, 0, 1), ("O", 1, 3, 1, "s"), ("MM", 2, 1, 1), ("O", 2, 0, 1, "v"), ("st", 1, 1), ("MM", 2, 2, 1),
-    ("O", 2, 1, 1, "s"), ("MM", 2, 3, 1), ("O", 2, 2, 1, "v"), ("MM", 3, 0, 1), ("O", 2, 3, 1, "s"), ("MM", 3, 1, 1),
-    ("O", 3, 0, 1, "v"), ("st", 2, 1), ("MM", 3, 2, 1), ("O", 3, 1, 1, "s"), ("MM", 3, 3, 1), ("O", 3, 2, 1, "v"),
-    ("MM", 4, 0, 0), ("O", 3, 3, 1, "s"), ("MM", 4, 0, 1), ("O", 4, 0, 0, "v"), ("st", 3, 1), ("MM", 4, 1, 0),
-    ("O", 4, 0, 1, "s"), ("MM", 4, 1, 1), ("O", 4, 1, 0, "v"), ("MM", 4, 2, 0), ("O", 4, 1, 1, "s"), ("MM", 4, 2, 1),
-    ("O", 4, 2, 0, "v"), ("st", 4, 0), ("MM", 4, 3, 0), ("O", 4, 2, 1, "s"), ("MM", 4, 3, 1), ("O", 4, 3, 0, "v"),
-    ("T", 6, 0), ("O", 4, 3, 1, "s"), ("T", 6, 1), ("Tc", 6, 0, "s"), ("T", 6, 2), ("st", 4, 1),
-    ("Tc", 6, 1, "v"), ("T", 6, 3), ("Tc", 6, 2, "s"), ("MM", 5, 0, 0), ("Tc", 6, 3, "s"), ("MM", 5, 0, 1),
-    ("O", 5, 0, 0, "v"), ("MM", 5, 1, 0), ("O", 5, 0, 1, "s"), ("qC", 6, 0), ("MM", 5, 1, 1), ("O", 5, 1, 0, "v"),
-    ("MM", 5, 2, 0), ("O", 5, 1, 1, "s"), ("qC", 6, 1), ("MM", 5, 2, 1), ("O", 5, 2, 0, "v"), ("st", 5, 0),
-    ("MM", 5, 3, 0), ("O", 5, 2, 1, "s"), ("MM", 5, 3, 1), ("O", 5, 3, 0, "v"), ("T", 7, 0), ("O", 5, 3, 1, "s"),
-    ("T", 7, 1), ("Tc", 7, 0, "s"), ("T", 7, 2), ("st", 5, 1), ("Tc", 7, 1, "v"), ("T", 7, 3),
-    ("Tc", 7, 2, "s"), ("MM", 6, 0, 0), ("Tc", 7, 3, "s"), ("MM", 6, 0, 1), ("O", 6, 0, 0, "v"), ("MM", 6, 1, 0),
-    ("O", 6, 0, 1, "s"), ("qC", 7, 0), ("MM", 6, 1, 1), ("O", 6, 1, 0, "v"), ("MM", 6, 2, 0), ("O", 6, 1, 1, "s"),
-    ("qC", 7, 1), ("MM", 6, 2, 1), ("O", 6, 2, 0, "v"), ("st", 6, 0), ("MM", 6, 3, 0), ("O", 6, 2, 1, "s"),
-    ("MM", 6, 3, 1), ("O", 6, 3, 0, "v"), ("MM", 7, 0, 0), ("O", 6, 3, 1, "s"), ("MM", 7, 0, 1), ("O", 7, 0, 0, "v"),
-    ("st", 6, 1), ("MM", 7, 1, 0), ("O", 7, 0, 1, "s"), ("MM", 7, 1, 1), ("O", 7, 1, 0, "v"), ("MM", 7, 2, 0),
-    ("O", 7, 1, 1, "s"), ("MM", 7, 2, 1), ("O", 7, 2, 0, "v"), ("st", 7, 0), ("MM", 7, 3, 0), ("O", 7, 2, 1, "s"),
-    ("MM", 7, 3, 1), ("O", 7, 3, 0, "v"), ("O", 7, 3, 1, "s"), ("st", 7, 1),
+    ("ms",), ("id",), ("lx", 1), ("lx", 0), ("lw", 0), ("lb",),
+    ("xT", 0), ("xT", 1), ("xT", 2), ("xT", 3), ("xc", 0, "s"), ("xc", 1, "v"),
+    ("xc", 2, "s"), ("xc", 3, "v"), ("qx", 0), ("lw", 1), ("R", 0, 0, "v"), ("lw", 2),
+    ("lw", 3), ("R", 0, 1, "v"), ("R", 1, 1, "v"), ("bm", 0), ("bm", 1), ("bm", 2),
+    ("bm", 3), ("bc", 0), ("bc", 1), ("bc", 2), ("bc", 3), ("qW", 0, 0),
+    ("lc", 0), ("R", 1, 0, "s"), ("qx", 1), ("qW", 1, 0), ("R", 2, 0, "s"), ("lc", 1),
+    ("qW", 0, 1), ("qW", 1, 1), ("R", 3, 0, "s"), ("S1", 0, 0, 0), ("S1", 0, 0, 1), ("S1", 0, 0, 2),
+    ("S1", 0, 0, 3), ("B", 0, 0, 0), ("B", 0, 0, 1), ("B", 0, 0, 2), ("B", 0, 0, 3), ("lc", 2),
+    ("qW", 2, 0), ("T", 0, 0), ("T", 0, 1), ("T", 0, 2), ("T", 0, 3), ("R", 2, 1, "s"),
+    ("qW", 3, 0), ("lc", 4), ("S1", 1, 0, 0), ("S1", 1, 0, 1), ("S1", 1, 0, 2), ("S1", 1, 0, 3),
+    ("lc", 5), ("qF", 0, 0), ("Tc", 0, 0, "s"), ("Tc", 0, 1, "s"), ("Tc", 0, 2, "s"), ("Tc", 0, 3, "s"),
+    ("T", 1, 0), ("T", 1, 1), ("T", 1, 2), ("T", 1, 3), ("B", 1, 0, 0), ("B", 1, 0, 1),
+    ("B", 1, 0, 2), ("B", 1, 0, 3), ("qC", 0, 1), ("lc", 3), ("lc", 6), ("T", 2, 0),
+    ("T", 2, 1), ("T", 2, 2), ("T", 2, 3), ("qC", 0, 0), ("qF", 1, 0), ("R", 3, 1, "v"),
+    ("qW", 3, 1), ("Tc", 1, 0, "s"), ("Tc", 1, 1, "s"), ("Tc", 1, 2, "s"), ("Tc", 1, 3, "s"), ("MM", 0, 0, 0),
+    ("MM", 0, 1, 0), ("MM", 0, 2, 0), ("MM", 0, 3, 0), ("Tc", 2, 0, "s"), ("Tc", 2, 1, "v"), ("Tc", 2, 2, "v"),
+    ("Tc", 2, 3, "s"), ("S1", 0, 1, 0), ("S1", 0, 1, 1), ("S1", 0, 1, 2), ("S1", 0, 1, 3), ("lc", 7),
+    ("T", 4, 0), ("T", 4, 1), ("T", 4, 2), ("T", 4, 3), ("qC", 1, 0), ("qC", 1, 1),
+    ("qW", 2, 1), ("O", 0, 0, 0, "s"), ("O", 0, 1, 0, "s"), ("O", 0, 2, 0, "s"), ("O", 0, 3, 0, "s"), ("MM", 1, 0, 0),
+    ("MM", 1, 1, 0), ("MM", 1, 2, 0), ("MM", 1, 3, 0), ("B", 0, 1, 0), ("B", 0, 1, 1), ("B", 0, 1, 2),
+    ("B", 0, 1, 3), ("Tc", 4, 0, "s"), ("Tc", 4, 1, "s"), ("Tc", 4, 2, "v"), ("Tc", 4, 3, "s"), ("qC", 2, 0),
+    ("qC", 2, 1), ("qF", 0, 1), ("O", 1, 0, 0, "s"), ("O", 1, 1, 0, "s"), ("O", 1, 2, 0, "s"), ("O", 1, 3, 0, "s"),
+    ("T", 3, 0), ("T", 3, 1), ("T", 3, 2), ("T", 3, 3), ("Tc", 3, 0, "s"), ("Tc", 3, 1, "v"),
+    ("Tc", 3, 2, "s"), ("Tc", 3, 3, "s"), ("MM", 2, 0, 0), ("MM", 2, 1, 0), ("MM", 2, 2, 0), ("MM", 2, 3, 0),
+    ("st", 1, 0), ("O", 2, 0, 0, "v"), ("O", 2, 1, 0, "v"), ("O", 2, 2, 0, "s"), ("O", 2, 3, 0, "s"), ("qC", 3, 0),
+    ("qC", 3, 1), ("S1", 1, 1, 0), ("S1", 1, 1, 1), ("S1", 1, 1, 2), ("S1", 1, 1, 3), ("B", 1, 1, 0),
+    ("B", 1, 1, 1), ("B", 1, 1, 2), ("B", 1, 1, 3), ("qF", 1, 1), ("T", 5, 0), ("T", 5, 1),
+    ("T", 5, 2), ("T", 5, 3), ("qC", 4, 0), ("qC", 4, 1), ("Tc", 5, 0, "s"), ("Tc", 5, 1, "s"),
+    ("Tc", 5, 2, "v"), ("Tc", 5, 3, "v"), ("MM", 3, 0, 0), ("MM", 3, 1, 0), ("MM", 3, 2, 0), ("MM", 3, 3, 0),
+    ("MM", 0, 0, 1), ("MM", 0, 1, 1), ("MM", 0, 2, 1), ("MM", 0, 3, 1), ("MM", 1, 0, 1), ("MM", 1, 1, 1),
+    ("MM", 1, 2, 1), ("MM", 1, 3, 1), ("st", 0, 0), ("O", 3, 0, 0, "s"), ("O", 3, 1, 0, "s"), ("O", 3, 2, 0, "s"),
+    ("O", 3, 3, 0, "s"), ("st", 2, 0), ("O", 0, 0, 1, "s"), ("O", 0, 1, 1, "s"), ("O", 0, 2, 1, "s"), ("O", 0, 3, 1, "v"),
+    ("O", 1, 0, 1, "s"), ("O", 1, 1, 1, "s"), ("O", 1, 2, 1, "s"), ("O", 1, 3, 1, "v"), ("st", 3, 0), ("st", 0, 1),
+    ("MM", 2, 0, 1), ("MM", 2, 1, 1), ("MM", 2, 2, 1), ("MM", 2, 3, 1), ("O", 2, 0, 1, "s"), ("O", 2, 1, 1, "s"),
+    ("O", 2, 2, 1, "s"), ("O", 2, 3, 1, "s"), ("st", 1, 1), ("st", 2, 1), ("MM", 4, 0, 0), ("O", 4, 0, 0, "v"),
+    ("MM", 4, 0, 1), ("O", 4, 0, 1, "s"), ("MM", 4, 1, 0), ("O", 4, 1, 0, "v"), ("MM", 4, 1, 1), ("O", 4, 1, 1, "s"),
+    ("st", 4, 0), ("MM", 4, 2, 0), ("O", 4, 2, 0, "v"), ("MM", 4, 2, 1), ("O", 4, 2, 1, "s"), ("MM", 4, 3, 0),
+    ("O", 4, 3, 0, "v"), ("MM", 4, 3, 1), ("O", 4, 3, 1, "s"), ("st", 4, 1), ("qC", 5, 0), ("qC", 5, 1),
+    ("MM", 3, 0, 1), ("MM", 3, 1, 1), ("MM", 3, 2, 1), ("MM", 3, 3, 1), ("O", 3, 0, 1, "v"), ("O", 3, 1, 1, "v"),
+    ("O", 3, 2, 1, "v"), ("O", 3, 3, 1, "s"), ("st", 3, 1), ("T", 6, 0), ("T", 6, 1), ("T", 6, 2),
+    ("T", 6, 3), ("Tc", 6, 0, "v"), ("Tc", 6, 1, "v"), ("Tc", 6, 2, "s"), ("Tc", 6, 3, "s"), ("MM", 5, 0, 0),
+    ("O", 5, 0, 0, "v"), ("MM", 5, 0, 1), ("O", 5, 0, 1, "s"), ("qC", 6, 0), ("MM", 5, 1, 0), ("O", 5, 1, 0, "v"),
+    ("MM", 5, 1, 1), ("O", 5, 1, 1, "s"), ("st", 5, 0), ("qC", 6, 1), ("MM", 5, 2, 0), ("O", 5, 2, 0, "v"),
+    ("MM", 5, 2, 1), ("O", 5, 2, 1, "s"), ("MM", 5, 3, 0), ("O", 5, 3, 0, "v"), ("MM", 5, 3, 1), ("O", 5, 3, 1, "s"),
+    ("st", 5, 1), ("T", 7, 0), ("T", 7, 1), ("T", 7, 2), ("T", 7, 3), ("Tc", 7, 0, "s"),
+    ("Tc", 7, 1, "s"), ("Tc", 7, 2, "v"), ("Tc", 7, 3, "v"), ("MM", 6, 0, 0), ("O", 6, 0, 0, "v"), ("MM", 6, 0, 1),
+    ("O", 6, 0, 1, "s"), ("st", 6, 0), ("qC", 7, 0), ("MM", 6, 1, 0), ("O", 6, 1, 0, "v"), ("MM", 6, 1, 1),
+    ("O", 6, 1, 1, "s"), ("st", 6, 1), ("qC", 7, 1), ("MM", 6, 2, 0), ("O", 6, 2, 0, "v"), ("MM", 6, 2, 1),
+    ("O", 6, 2, 1, "s"), ("st", 6, 2), ("MM", 6, 3, 0), ("O", 6, 3, 0, "v"), ("MM", 6, 3, 1), ("O", 6, 3, 1, "s"),
+    ("st", 6, 3), ("MM", 7, 0, 0), ("O", 7, 0, 0, "v"), ("MM", 7, 0, 1), ("O", 7, 0, 1, "s"), ("st", 7, 0),
+    ("MM", 7, 1, 0), ("O", 7, 1, 0, "v"), ("MM", 7, 1, 1), ("O", 7, 1, 1, "s"), ("st", 7, 1), ("MM", 7, 2, 0),
+    ("O", 7, 2, 0, "v"), ("MM", 7, 2, 1), ("O", 7, 2, 1, "s"), ("st", 7, 2), ("MM", 7, 3, 0), ("O", 7, 3, 0, "v"),
+    ("MM", 7, 3, 1), ("O", 7, 3, 1, "s"), ("st", 7, 3),
 )
 
 
@@ -110,7 +114,7 @@ def tile_expertparallelbehindblock_t_kernel(tc, x_in, cw_in, w_in, b_in, out):
 
         def op_ms():
             big("brow", [P, E * D_OUT], BF16)
-            nc.vector.memset(t["brow"][:], 0.0)
+            nc.vector.memset(t["brow"][:].bitcast(I32), 0)
             nc.vector.memset(ones[:], 1.0)
 
         def op_id():
@@ -119,11 +123,12 @@ def tile_expertparallelbehindblock_t_kernel(tc, x_in, cw_in, w_in, b_in, out):
         def op_lb():
             nc.sync.dma_start(out=t["brow"][0:1, :], in_=b_in.rearrange("e o d -> o (e d)"))
 
-        def op_lx():
-            big("x", [P, 8, D_IN], BF16)
+        def op_lx(h):
+            if "x" not in t:
+                big("x", [P, 8, D_IN], BF16)
             nc.sync.dma_start(
-                out=t["x"][:].rearrange("p (a e) k -> p a e k", e=2),
-                in_=x_in.rearrange("(a p e) k -> p a e k", a=E, e=2),
+                out=t["x"][:, 4 * h : 4 * h + 4, :].rearrange("p (a e) k -> p a e k", e=2),
+                in_=x_in[512 * h : 512 * (h + 1), :].rearrange("(a p e) k -> p a e k", a=2, e=2),
             )
 
         def op_lw(a):
@@ -134,7 +139,7 @@ def tile_expertparallelbehindblock_t_kernel(tc, x_in, cw_in, w_in, b_in, out):
             )
 
         def op_lc(c):
-            t["cw%d" % c] = rot.tile([P, 4, 1024], BF16, tag="cw", bufs=7, name="cw%d" % c)
+            t["cw%d" % c] = rot.tile([P, 4, 1024], BF16, tag="cw", bufs=6, name="cw%d" % c)
             nc.sync.dma_start(out=t["cw%d" % c][:], in_=cw_rows[c])
 
         def op_bm(a):
@@ -174,7 +179,7 @@ def tile_expertparallelbehindblock_t_kernel(tc, x_in, cw_in, w_in, b_in, out):
             )
 
         def op_R(a, n, eng):
-            g_t = rot.tile([P, 2048], BF16, tag="wg", bufs=5, align_bytes=64, name="wg%d%d" % (a, n))
+            g_t = rot.tile([P, 2048], BF16, tag="wg", bufs=6, align_bytes=64, name="wg%d%d" % (a, n))
             t["wg%d%d" % (a, n)] = g_t
             copy_on(
                 eng,
@@ -207,7 +212,7 @@ def tile_expertparallelbehindblock_t_kernel(tc, x_in, cw_in, w_in, b_in, out):
         def op_B(g, n, d):
             key = "fg%d%d" % (g, n)
             if key not in t:
-                t[key] = rot.tile([P, 512, 4], BF16, tag="wg", bufs=5, align_bytes=64, name=key)
+                t[key] = rot.tile([P, 512, 4], BF16, tag="fg", bufs=4, align_bytes=64, name=key)
             cols = slice((4 * n + d) * P, (4 * n + d + 1) * P)
             nc.vector.tensor_tensor(
                 out=t[key][:, d * P : (d + 1) * P, :].rearrange("p d (u e) -> p d u e", e=2),
@@ -232,11 +237,11 @@ def tile_expertparallelbehindblock_t_kernel(tc, x_in, cw_in, w_in, b_in, out):
                 nc.tensor.transpose(ct[:, a, :], cw_w[:, j, a * P : (a + 1) * P], ident[:])
 
         def op_Tc(c, j, eng):
-            key = "cwg%d" % c
+            key = "cwg%d%d" % (c, j // 2)
             if key not in t:
-                t[key] = rot.tile([P, 4096], BF16, tag="cwg", bufs=3, align_bytes=64, name=key)
-            cwg_w = t[key][:].bitcast(F32).rearrange("p (j g s u) -> p j g s u", j=4, g=2, u=2)
-            copy_on(eng, cwg_w[:, j], t["ct%d%d" % (c, j)][:].rearrange("p (g u) s -> p g s u", u=2))
+                t[key] = rot.tile([P, 2048], BF16, tag="cwg", bufs=5, align_bytes=64, name=key)
+            cwg_w = t[key][:].bitcast(F32).rearrange("p (j g s u) -> p j g s u", j=2, g=2, u=2)
+            copy_on(eng, cwg_w[:, j % 2], t["ct%d%d" % (c, j)][:].rearrange("p (g u) s -> p g s u", u=2))
 
         def op_qC(c, h):
             key = "cwq%d" % c
@@ -246,7 +251,7 @@ def tile_expertparallelbehindblock_t_kernel(tc, x_in, cw_in, w_in, b_in, out):
             nc.vector.quantize_mx(
                 out=t[key][:, h * 512 : (h + 1) * 512].bitcast(FP8X4),
                 scales=t["cws%d" % c][:, h * 512 : (h + 1) * 512],
-                in_=t["cwg%d" % c][:, h * 2048 : (h + 1) * 2048],
+                in_=t["cwg%d%d" % (c, h)][:],
             )
 
         def op_MM(c, j, n):
@@ -271,6 +276,11 @@ def tile_expertparallelbehindblock_t_kernel(tc, x_in, cw_in, w_in, b_in, out):
                 if key not in t:
                     big(key, [P, 4, 512], F32)
                 copy_on(eng, t[key][:, j, :], acc[:])
+            elif c in FINE:
+                key = "o%dj%d" % (c, j)
+                if key not in t:
+                    big(key, [P, D_OUT], F32)
+                copy_on(eng, t[key][:, n * 512 : (n + 1) * 512], acc[:])
             else:
                 key = "o%dh%d" % (c, j // 2)
                 if key not in t:
@@ -280,6 +290,8 @@ def tile_expertparallelbehindblock_t_kernel(tc, x_in, cw_in, w_in, b_in, out):
         def op_st(c, x):
             if c < KE:
                 nc.sync.dma_start(out=out_rows[c][:, :, x * 512 : (x + 1) * 512], in_=t["o%dn%d" % (c, x)][:])
+            elif c in FINE:
+                nc.sync.dma_start(out=out_rows[c][:, x, :], in_=t["o%dj%d" % (c, x)][:])
             else:
                 nc.sync.dma_start(out=out_rows[c][:, 2 * x : 2 * x + 2, :], in_=t["o%dh%d" % (c, x)][:])
 

@@ -5,300 +5,318 @@ from concourse.masks import make_identity
 
 F32 = mybir.dt.float32
 BF16 = mybir.dt.bfloat16
+I32 = mybir.dt.int32
 U32 = mybir.dt.uint32
 U8 = mybir.dt.uint8
-I32 = mybir.dt.int32
 FP8X4 = mybir.dt.float8_e4m3fn_x4
 ADD = mybir.AluOpType.add
 
 P = 128
-E = 4
+EXPERTS = 4
 D_IN = 512
 D_OUT = 1024
-FLOPS = 2 * 1024 * 512 * 1024 + 2 * 4096 * 1024 * 1024
-KE = 4
-PINNED = True
-
-FINE = (6, 7)
-
-ORDER = (
-    ("ms",), ("id",), ("lx", 1), ("lx", 0), ("lw", 0), ("lb",),
-    ("xT", 0), ("xT", 1), ("xT", 2), ("xT", 3), ("xc", 0, "s"), ("xc", 1, "v"),
-    ("xc", 2, "s"), ("xc", 3, "v"), ("qx", 0), ("lw", 1), ("R", 0, 0, "v"), ("lw", 2),
-    ("lw", 3), ("R", 0, 1, "v"), ("R", 1, 1, "v"), ("bm", 0), ("bm", 1), ("bm", 2),
-    ("bm", 3), ("bc", 0), ("bc", 1), ("bc", 2), ("bc", 3), ("qW", 0, 0),
-    ("lc", 0), ("R", 1, 0, "s"), ("qx", 1), ("qW", 1, 0), ("R", 2, 0, "s"), ("lc", 1),
-    ("qW", 0, 1), ("qW", 1, 1), ("R", 3, 0, "s"), ("S1", 0, 0, 0), ("S1", 0, 0, 1), ("S1", 0, 0, 2),
-    ("S1", 0, 0, 3), ("B", 0, 0, 0), ("B", 0, 0, 1), ("B", 0, 0, 2), ("B", 0, 0, 3), ("lc", 2),
-    ("qW", 2, 0), ("T", 0, 0), ("T", 0, 1), ("T", 0, 2), ("T", 0, 3), ("R", 2, 1, "s"),
-    ("qW", 3, 0), ("lc", 4), ("S1", 1, 0, 0), ("S1", 1, 0, 1), ("S1", 1, 0, 2), ("S1", 1, 0, 3),
-    ("lc", 5), ("qF", 0, 0), ("Tc", 0, 0, "s"), ("Tc", 0, 1, "s"), ("Tc", 0, 2, "s"), ("Tc", 0, 3, "s"),
-    ("T", 1, 0), ("T", 1, 1), ("T", 1, 2), ("T", 1, 3), ("B", 1, 0, 0), ("B", 1, 0, 1),
-    ("B", 1, 0, 2), ("B", 1, 0, 3), ("qC", 0, 1), ("lc", 3), ("lc", 6), ("T", 2, 0),
-    ("T", 2, 1), ("T", 2, 2), ("T", 2, 3), ("qC", 0, 0), ("qF", 1, 0), ("R", 3, 1, "v"),
-    ("qW", 3, 1), ("Tc", 1, 0, "s"), ("Tc", 1, 1, "s"), ("Tc", 1, 2, "s"), ("Tc", 1, 3, "s"), ("MM", 0, 0, 0),
-    ("MM", 0, 1, 0), ("MM", 0, 2, 0), ("MM", 0, 3, 0), ("Tc", 2, 0, "s"), ("Tc", 2, 1, "v"), ("Tc", 2, 2, "v"),
-    ("Tc", 2, 3, "s"), ("S1", 0, 1, 0), ("S1", 0, 1, 1), ("S1", 0, 1, 2), ("S1", 0, 1, 3), ("lc", 7),
-    ("T", 4, 0), ("T", 4, 1), ("T", 4, 2), ("T", 4, 3), ("qC", 1, 0), ("qC", 1, 1),
-    ("qW", 2, 1), ("O", 0, 0, 0, "s"), ("O", 0, 1, 0, "s"), ("O", 0, 2, 0, "s"), ("O", 0, 3, 0, "s"), ("MM", 1, 0, 0),
-    ("MM", 1, 1, 0), ("MM", 1, 2, 0), ("MM", 1, 3, 0), ("B", 0, 1, 0), ("B", 0, 1, 1), ("B", 0, 1, 2),
-    ("B", 0, 1, 3), ("Tc", 4, 0, "s"), ("Tc", 4, 1, "s"), ("Tc", 4, 2, "v"), ("Tc", 4, 3, "s"), ("qC", 2, 0),
-    ("qC", 2, 1), ("qF", 0, 1), ("O", 1, 0, 0, "s"), ("O", 1, 1, 0, "s"), ("O", 1, 2, 0, "s"), ("O", 1, 3, 0, "s"),
-    ("T", 3, 0), ("T", 3, 1), ("T", 3, 2), ("T", 3, 3), ("Tc", 3, 0, "s"), ("Tc", 3, 1, "v"),
-    ("Tc", 3, 2, "s"), ("Tc", 3, 3, "s"), ("MM", 2, 0, 0), ("MM", 2, 1, 0), ("MM", 2, 2, 0), ("MM", 2, 3, 0),
-    ("st", 1, 0), ("O", 2, 0, 0, "v"), ("O", 2, 1, 0, "v"), ("O", 2, 2, 0, "s"), ("O", 2, 3, 0, "s"), ("qC", 3, 0),
-    ("qC", 3, 1), ("S1", 1, 1, 0), ("S1", 1, 1, 1), ("S1", 1, 1, 2), ("S1", 1, 1, 3), ("B", 1, 1, 0),
-    ("B", 1, 1, 1), ("B", 1, 1, 2), ("B", 1, 1, 3), ("qF", 1, 1), ("T", 5, 0), ("T", 5, 1),
-    ("T", 5, 2), ("T", 5, 3), ("qC", 4, 0), ("qC", 4, 1), ("Tc", 5, 0, "s"), ("Tc", 5, 1, "s"),
-    ("Tc", 5, 2, "v"), ("Tc", 5, 3, "v"), ("MM", 3, 0, 0), ("MM", 3, 1, 0), ("MM", 3, 2, 0), ("MM", 3, 3, 0),
-    ("MM", 0, 0, 1), ("MM", 0, 1, 1), ("MM", 0, 2, 1), ("MM", 0, 3, 1), ("MM", 1, 0, 1), ("MM", 1, 1, 1),
-    ("MM", 1, 2, 1), ("MM", 1, 3, 1), ("st", 0, 0), ("O", 3, 0, 0, "s"), ("O", 3, 1, 0, "s"), ("O", 3, 2, 0, "s"),
-    ("O", 3, 3, 0, "s"), ("st", 2, 0), ("O", 0, 0, 1, "s"), ("O", 0, 1, 1, "s"), ("O", 0, 2, 1, "s"), ("O", 0, 3, 1, "v"),
-    ("O", 1, 0, 1, "s"), ("O", 1, 1, 1, "s"), ("O", 1, 2, 1, "s"), ("O", 1, 3, 1, "v"), ("st", 3, 0), ("st", 0, 1),
-    ("MM", 2, 0, 1), ("MM", 2, 1, 1), ("MM", 2, 2, 1), ("MM", 2, 3, 1), ("O", 2, 0, 1, "s"), ("O", 2, 1, 1, "s"),
-    ("O", 2, 2, 1, "s"), ("O", 2, 3, 1, "s"), ("st", 1, 1), ("st", 2, 1), ("MM", 4, 0, 0), ("O", 4, 0, 0, "v"),
-    ("MM", 4, 0, 1), ("O", 4, 0, 1, "s"), ("MM", 4, 1, 0), ("O", 4, 1, 0, "v"), ("MM", 4, 1, 1), ("O", 4, 1, 1, "s"),
-    ("st", 4, 0), ("MM", 4, 2, 0), ("O", 4, 2, 0, "v"), ("MM", 4, 2, 1), ("O", 4, 2, 1, "s"), ("MM", 4, 3, 0),
-    ("O", 4, 3, 0, "v"), ("MM", 4, 3, 1), ("O", 4, 3, 1, "s"), ("st", 4, 1), ("qC", 5, 0), ("qC", 5, 1),
-    ("MM", 3, 0, 1), ("MM", 3, 1, 1), ("MM", 3, 2, 1), ("MM", 3, 3, 1), ("O", 3, 0, 1, "v"), ("O", 3, 1, 1, "v"),
-    ("O", 3, 2, 1, "v"), ("O", 3, 3, 1, "s"), ("st", 3, 1), ("T", 6, 0), ("T", 6, 1), ("T", 6, 2),
-    ("T", 6, 3), ("Tc", 6, 0, "v"), ("Tc", 6, 1, "v"), ("Tc", 6, 2, "s"), ("Tc", 6, 3, "s"), ("MM", 5, 0, 0),
-    ("O", 5, 0, 0, "v"), ("MM", 5, 0, 1), ("O", 5, 0, 1, "s"), ("qC", 6, 0), ("MM", 5, 1, 0), ("O", 5, 1, 0, "v"),
-    ("MM", 5, 1, 1), ("O", 5, 1, 1, "s"), ("st", 5, 0), ("qC", 6, 1), ("MM", 5, 2, 0), ("O", 5, 2, 0, "v"),
-    ("MM", 5, 2, 1), ("O", 5, 2, 1, "s"), ("MM", 5, 3, 0), ("O", 5, 3, 0, "v"), ("MM", 5, 3, 1), ("O", 5, 3, 1, "s"),
-    ("st", 5, 1), ("T", 7, 0), ("T", 7, 1), ("T", 7, 2), ("T", 7, 3), ("Tc", 7, 0, "s"),
-    ("Tc", 7, 1, "s"), ("Tc", 7, 2, "v"), ("Tc", 7, 3, "v"), ("MM", 6, 0, 0), ("O", 6, 0, 0, "v"), ("MM", 6, 0, 1),
-    ("O", 6, 0, 1, "s"), ("st", 6, 0), ("qC", 7, 0), ("MM", 6, 1, 0), ("O", 6, 1, 0, "v"), ("MM", 6, 1, 1),
-    ("O", 6, 1, 1, "s"), ("st", 6, 1), ("qC", 7, 1), ("MM", 6, 2, 0), ("O", 6, 2, 0, "v"), ("MM", 6, 2, 1),
-    ("O", 6, 2, 1, "s"), ("st", 6, 2), ("MM", 6, 3, 0), ("O", 6, 3, 0, "v"), ("MM", 6, 3, 1), ("O", 6, 3, 1, "s"),
-    ("st", 6, 3), ("MM", 7, 0, 0), ("O", 7, 0, 0, "v"), ("MM", 7, 0, 1), ("O", 7, 0, 1, "s"), ("st", 7, 0),
-    ("MM", 7, 1, 0), ("O", 7, 1, 0, "v"), ("MM", 7, 1, 1), ("O", 7, 1, 1, "s"), ("st", 7, 1), ("MM", 7, 2, 0),
-    ("O", 7, 2, 0, "v"), ("MM", 7, 2, 1), ("O", 7, 2, 1, "s"), ("st", 7, 2), ("MM", 7, 3, 0), ("O", 7, 3, 0, "v"),
-    ("MM", 7, 3, 1), ("O", 7, 3, 1, "s"), ("st", 7, 3),
-)
+HALF = 512
+SUPER_TILES = 8
+EARLY = 4
+FLOPS = 2 * 1024 * D_IN * D_OUT + 2 * 4096 * 1024 * D_OUT
 
 
-def tile_expertparallelbehindblock_t_kernel(tc, x_in, cw_in, w_in, b_in, out):
+def tile_expertparallelbehindblock_t_kernel(tc, inputs, combine_weights, weight, bias, out):
     nc = tc.nc
     with ExitStack() as ctx:
         keep = ctx.enter_context(tc.tile_pool(name="keep", bufs=1))
         rot = ctx.enter_context(tc.tile_pool(name="rot", bufs=1))
         psum = ctx.enter_context(tc.psum_pool(name="psum", bufs=4))
-        if PINNED:
-            ctx.enter_context(tc.manual_schedule())
+        ctx.enter_context(tc.manual_schedule())
 
-        cw_rows = cw_in.rearrange("(c p j) e k -> c p j (e k)", p=P, j=4)
+        cw_rows = combine_weights.rearrange("(c p j) e k -> c p j (e k)", p=P, j=4)
         out_rows = out.rearrange("b (h p j) d -> (b h) p j d", p=P, j=4)
 
         ident = keep.tile([P, P], F32)
         ones = keep.tile([P, P], BF16)
-        bias_bc = keep.tile([P, E, D_OUT], BF16)
-        xq = keep.tile([P, 1024], U32, align_bytes=64)
-        xs = keep.tile([P, 1024], U8, align_bytes=64)
-        wq = keep.tile([P, E, D_OUT], U32, align_bytes=64)
-        ws = keep.tile([P, E, D_OUT], U8, align_bytes=64)
-        fq = keep.tile([P, 2, D_OUT], U32, align_bytes=64)
-        fs = keep.tile([P, 2, D_OUT], U8, align_bytes=64)
+        bias_all = keep.tile([P, EXPERTS, D_OUT], BF16)
+        x_codes = keep.tile([P, 8 * P], U32, align_bytes=64)
+        x_scales = keep.tile([P, 8 * P], U8, align_bytes=64)
+        w_codes = keep.tile([P, EXPERTS, D_OUT], U32, align_bytes=64)
+        w_scales = keep.tile([P, EXPERTS, D_OUT], U8, align_bytes=64)
+        f_codes = keep.tile([P, 2, D_OUT], U32, align_bytes=64)
+        f_scales = keep.tile([P, 2, D_OUT], U8, align_bytes=64)
 
-        t = {}
+        live = {}
 
-        def big(name, shape, dtype):
-            t[name] = rot.tile(shape, dtype, tag="big", bufs=7, align_bytes=64, name=name)
-            return t[name]
+        def big_tile(name, shape, dtype):
+            live[name] = rot.tile(shape, dtype, tag="big", bufs=7, align_bytes=64, name=name)
+            return live[name]
 
-        def copy_on(eng, dst, src):
-            if eng == "v":
+        def copy_on(engine, dst, src):
+            if engine == "v":
                 nc.vector.tensor_copy(out=dst, in_=src)
             else:
                 nc.scalar.copy(out=dst, in_=src)
 
-        def op_ms():
-            big("brow", [P, E * D_OUT], BF16)
-            nc.vector.memset(t["brow"][:].bitcast(I32), 0)
+        def load_x(h):
+            if "x" not in live:
+                big_tile("x", [P, 8, D_IN], BF16)
+            nc.sync.dma_start(
+                out=live["x"][:, 4 * h : 4 * h + 4, :].rearrange("p (a e) k -> p a e k", e=2),
+                in_=inputs[512 * h : 512 * (h + 1), :].rearrange("(a p e) k -> p a e k", a=2, e=2),
+            )
+
+        def load_w(a):
+            raw = big_tile("w%d" % a, [P, 4, D_OUT], BF16)
+            nc.sync.dma_start(
+                out=raw[:].rearrange("p (u e) d -> p u e d", e=2),
+                in_=weight[a].rearrange("(u q e) d -> q u e d", u=2, e=2),
+            )
+
+        def load_cw(c):
+            live["cw%d" % c] = rot.tile([P, 4, 1024], BF16, tag="cw", bufs=6, name="cw%d" % c)
+            nc.sync.dma_start(out=live["cw%d" % c][:], in_=cw_rows[c])
+
+        def zero_bias_row():
+            big_tile("bias_row", [P, EXPERTS * D_OUT], BF16)
+            nc.vector.memset(live["bias_row"][:].bitcast(I32), 0)
             nc.vector.memset(ones[:], 1.0)
 
-        def op_id():
-            make_identity(nc, ident[:])
+        def load_bias():
+            nc.sync.dma_start(out=live["bias_row"][0:1, :], in_=bias.rearrange("e o d -> o (e d)"))
 
-        def op_lb():
-            nc.sync.dma_start(out=t["brow"][0:1, :], in_=b_in.rearrange("e o d -> o (e d)"))
-
-        def op_lx(h):
-            if "x" not in t:
-                big("x", [P, 8, D_IN], BF16)
-            nc.sync.dma_start(
-                out=t["x"][:, 4 * h : 4 * h + 4, :].rearrange("p (a e) k -> p a e k", e=2),
-                in_=x_in[512 * h : 512 * (h + 1), :].rearrange("(a p e) k -> p a e k", a=2, e=2),
-            )
-
-        def op_lw(a):
-            w_t = big("w%d" % a, [P, 4, D_OUT], BF16)
-            nc.sync.dma_start(
-                out=w_t[:].rearrange("p (u e) d -> p u e d", e=2),
-                in_=w_in[a].rearrange("(u q e) d -> q u e d", u=2, e=2),
-            )
-
-        def op_lc(c):
-            t["cw%d" % c] = rot.tile([P, 4, 1024], BF16, tag="cw", bufs=6, name="cw%d" % c)
-            nc.sync.dma_start(out=t["cw%d" % c][:], in_=cw_rows[c])
-
-        def op_bm(a):
-            bp = psum.tile([P, D_OUT], BF16, tag="acc", name="bp%d" % a)
-            t["bp%d" % a] = bp
-            for h in range(2):
-                nc.tensor.matmul(
-                    bp[:, h * 512 : (h + 1) * 512],
-                    lhsT=ones[:],
-                    rhs=t["brow"][:, a * D_OUT + h * 512 : a * D_OUT + (h + 1) * 512],
-                    start=True,
-                    stop=True,
-                )
-
-        def op_bc(a):
-            nc.scalar.copy(out=bias_bc[:, a, :], in_=t["bp%d" % a][:])
-
-        def op_xT(i):
-            xt = psum.tile([P, 2, 2, P], F32, tag="tr", name="xt%d" % i)
-            t["xt%d" % i] = xt
-            x_w = t["x"][:].bitcast(F32)
-            for i2 in range(2):
-                for u in range(2):
-                    nc.tensor.transpose(xt[:, i2, u, :], x_w[:, 2 * i + i2, u * P : (u + 1) * P], ident[:])
-
-        def op_xc(i, eng):
-            if "xg" not in t:
-                big("xg", [P, 4096], BF16)
-            xg_w = t["xg"][:].bitcast(F32).rearrange("p (i s u) -> p i s u", i=8, u=2)
-            copy_on(eng, xg_w[:, 2 * i : 2 * i + 2, :, :], t["xt%d" % i][:].rearrange("p i u s -> p i s u"))
-
-        def op_qx(h):
-            nc.vector.quantize_mx(
-                out=xq[:, h * 512 : (h + 1) * 512].bitcast(FP8X4),
-                scales=xs[:, h * 512 : (h + 1) * 512],
-                in_=t["xg"][:, h * 2048 : (h + 1) * 2048],
-            )
-
-        def op_R(a, n, eng):
-            g_t = rot.tile([P, 2048], BF16, tag="wg", bufs=6, align_bytes=64, name="wg%d%d" % (a, n))
-            t["wg%d%d" % (a, n)] = g_t
-            copy_on(
-                eng,
-                g_t[:].rearrange("p (c i t) -> p c t i", i=4, t=4),
-                t["w%d" % a][:, :, n * 512 : (n + 1) * 512].rearrange("p t (c i) -> p c t i", i=4),
-            )
-
-        def op_qW(a, n):
-            cols = slice(n * 512, (n + 1) * 512)
-            nc.vector.quantize_mx(out=wq[:, a, cols].bitcast(FP8X4), scales=ws[:, a, cols], in_=t["wg%d%d" % (a, n)][:])
-
-        def op_S1(g, n, d):
-            cols = slice((4 * n + d) * P, (4 * n + d + 1) * P)
-            fp = psum.tile([P, 2, 2, P], F32, tag="acc", name="fp%d%d%d" % (g, n, d))
-            t["fp%d%d%d" % (g, n, d)] = fp
-            for u in range(2):
-                a = 2 * g + u
-                for e in range(2):
-                    xc = slice((2 * a + e) * P, (2 * a + e + 1) * P)
-                    nc.tensor.matmul_mx(
-                        out=fp[:, u, e, :],
-                        lhsT=xq[:, xc].bitcast(FP8X4),
-                        lhsT_scale=xs[:, xc],
-                        rhs=wq[:, a, cols].bitcast(FP8X4),
-                        rhs_scale=ws[:, a, cols],
-                        start=True,
-                        stop=True,
+        def spread_bias():
+            for a in range(EXPERTS):
+                bank = psum.tile([P, D_OUT], BF16, tag="acc", name="bias_ps%d" % a)
+                live["bias_ps%d" % a] = bank
+                for h in range(2):
+                    cols = slice(a * D_OUT + h * HALF, a * D_OUT + (h + 1) * HALF)
+                    nc.tensor.matmul(
+                        bank[:, h * HALF : (h + 1) * HALF], lhsT=ones[:], rhs=live["bias_row"][:, cols], start=True, stop=True
                     )
 
-        def op_B(g, n, d):
-            key = "fg%d%d" % (g, n)
-            if key not in t:
-                t[key] = rot.tile([P, 512, 4], BF16, tag="fg", bufs=4, align_bytes=64, name=key)
-            cols = slice((4 * n + d) * P, (4 * n + d + 1) * P)
-            nc.vector.tensor_tensor(
-                out=t[key][:, d * P : (d + 1) * P, :].rearrange("p d (u e) -> p d u e", e=2),
-                in0=t["fp%d%d%d" % (g, n, d)][:].rearrange("p u e d -> p d u e"),
-                in1=bias_bc[:, 2 * g : 2 * g + 2, cols].rearrange("p u d -> p d u").unsqueeze(3).to_broadcast([P, P, 2, 2]),
-                op=ADD,
-            )
+        def copy_bias():
+            for a in range(EXPERTS):
+                nc.scalar.copy(out=bias_all[:, a, :], in_=live["bias_ps%d" % a][:])
 
-        def op_qF(g, n):
-            cols = slice(n * 512, (n + 1) * 512)
+        def transpose_x():
+            words = live["x"][:].bitcast(F32)
+            for i in range(4):
+                bank = psum.tile([P, 2, 2, P], F32, tag="tr", name="x_ps%d" % i)
+                live["x_ps%d" % i] = bank
+                for i2 in range(2):
+                    for u in range(2):
+                        nc.tensor.transpose(bank[:, i2, u, :], words[:, 2 * i + i2, u * P : (u + 1) * P], ident[:])
+
+        def copy_x(engines):
+            big_tile("x_grouped", [P, 4096], BF16)
+            words = live["x_grouped"][:].bitcast(F32).rearrange("p (i s u) -> p i s u", i=8, u=2)
+            for i in range(4):
+                copy_on(engines[i], words[:, 2 * i : 2 * i + 2, :, :], live["x_ps%d" % i][:].rearrange("p i u s -> p i s u"))
+
+        def quantise_x(g):
             nc.vector.quantize_mx(
-                out=fq[:, g, cols].bitcast(FP8X4),
-                scales=fs[:, g, cols],
-                in_=t["fg%d%d" % (g, n)][:].rearrange("p d t -> p (d t)"),
+                out=x_codes[:, g * 512 : (g + 1) * 512].bitcast(FP8X4),
+                scales=x_scales[:, g * 512 : (g + 1) * 512],
+                in_=live["x_grouped"][:, g * 2048 : (g + 1) * 2048],
             )
 
-        def op_T(c, j):
-            ct = psum.tile([P, 4, P], F32, tag="tr", name="ct%d%d" % (c, j))
-            t["ct%d%d" % (c, j)] = ct
-            cw_w = t["cw%d" % c][:].bitcast(F32)
-            for a in range(4):
-                nc.tensor.transpose(ct[:, a, :], cw_w[:, j, a * P : (a + 1) * P], ident[:])
+        def regroup_w(a, n, engine):
+            grouped = rot.tile([P, 4 * HALF], BF16, tag="w_grouped", bufs=6, align_bytes=64, name="wg%d%d" % (a, n))
+            live["wg%d%d" % (a, n)] = grouped
+            copy_on(
+                engine,
+                grouped[:].rearrange("p (c i t) -> p c t i", i=4, t=4),
+                live["w%d" % a][:, :, n * HALF : (n + 1) * HALF].rearrange("p t (c i) -> p c t i", i=4),
+            )
 
-        def op_Tc(c, j, eng):
-            key = "cwg%d%d" % (c, j // 2)
-            if key not in t:
-                t[key] = rot.tile([P, 2048], BF16, tag="cwg", bufs=5, align_bytes=64, name=key)
-            cwg_w = t[key][:].bitcast(F32).rearrange("p (j g s u) -> p j g s u", j=2, g=2, u=2)
-            copy_on(eng, cwg_w[:, j % 2], t["ct%d%d" % (c, j)][:].rearrange("p (g u) s -> p g s u", u=2))
-
-        def op_qC(c, h):
-            key = "cwq%d" % c
-            if key not in t:
-                t[key] = rot.tile([P, 1024], U32, tag="cwq", bufs=5, align_bytes=64, name=key)
-                t["cws%d" % c] = rot.tile([P, 1024], U8, tag="cws", bufs=5, align_bytes=64, name="cws%d" % c)
+        def quantise_w(a, n):
+            cols = slice(n * HALF, (n + 1) * HALF)
             nc.vector.quantize_mx(
-                out=t[key][:, h * 512 : (h + 1) * 512].bitcast(FP8X4),
-                scales=t["cws%d" % c][:, h * 512 : (h + 1) * 512],
-                in_=t["cwg%d%d" % (c, h)][:],
+                out=w_codes[:, a, cols].bitcast(FP8X4), scales=w_scales[:, a, cols], in_=live["wg%d%d" % (a, n)][:]
             )
 
-        def op_MM(c, j, n):
-            acc = psum.tile([P, 512], F32, tag="acc", name="acc%d%d%d" % (c, j, n))
-            t["acc%d%d%d" % (c, j, n)] = acc
+        def stage1_passes(g, n):
+            for d in range(4 * n, 4 * n + 4):
+                cols = slice(d * P, (d + 1) * P)
+                bank = psum.tile([P, 2, 2, P], F32, tag="acc", name="f_ps%d%d" % (g, d))
+                live["f_ps%d%d" % (g, d)] = bank
+                for u in range(2):
+                    a = 2 * g + u
+                    for e in range(2):
+                        slots = slice((2 * a + e) * P, (2 * a + e + 1) * P)
+                        nc.tensor.matmul_mx(
+                            out=bank[:, u, e, :],
+                            lhsT=x_codes[:, slots].bitcast(FP8X4),
+                            lhsT_scale=x_scales[:, slots],
+                            rhs=w_codes[:, a, cols].bitcast(FP8X4),
+                            rhs_scale=w_scales[:, a, cols],
+                            start=True,
+                            stop=True,
+                        )
+
+        def stage1_bias(g, n):
+            grouped = rot.tile([P, HALF, 4], BF16, tag="f_grouped", bufs=4, align_bytes=64, name="fg%d%d" % (g, n))
+            live["fg%d%d" % (g, n)] = grouped
+            for d in range(4 * n, 4 * n + 4):
+                cols = slice(d * P, (d + 1) * P)
+                b_view = bias_all[:, 2 * g : 2 * g + 2, cols].rearrange("p u d -> p d u").unsqueeze(3)
+                nc.vector.tensor_tensor(
+                    out=grouped[:, (d - 4 * n) * P : (d - 4 * n + 1) * P, :].rearrange("p d (u e) -> p d u e", e=2),
+                    in0=live["f_ps%d%d" % (g, d)][:].rearrange("p u e d -> p d u e"),
+                    in1=b_view.to_broadcast([P, P, 2, 2]),
+                    op=ADD,
+                )
+
+        def quantise_flat(g, n):
+            cols = slice(n * HALF, (n + 1) * HALF)
+            nc.vector.quantize_mx(
+                out=f_codes[:, g, cols].bitcast(FP8X4),
+                scales=f_scales[:, g, cols],
+                in_=live["fg%d%d" % (g, n)][:].rearrange("p d t -> p (d t)"),
+            )
+
+        def transpose_cw(c):
+            words = live["cw%d" % c][:].bitcast(F32)
+            for j in range(4):
+                bank = psum.tile([P, 4, P], F32, tag="tr", name="cw_ps%d%d" % (c, j))
+                live["cw_ps%d%d" % (c, j)] = bank
+                for a in range(4):
+                    nc.tensor.transpose(bank[:, a, :], words[:, j, a * P : (a + 1) * P], ident[:])
+
+        def copy_cw(c, engines):
+            for j in range(4):
+                key = "cwg%d%d" % (c, j // 2)
+                if key not in live:
+                    live[key] = rot.tile([P, 2048], BF16, tag="cw_grouped", bufs=5, align_bytes=64, name=key)
+                words = live[key][:].bitcast(F32).rearrange("p (j g s u) -> p j g s u", j=2, g=2, u=2)
+                copy_on(engines[j], words[:, j % 2], live["cw_ps%d%d" % (c, j)][:].rearrange("p (g u) s -> p g s u", u=2))
+
+        def quantise_cw(c, h):
+            if "cwq%d" % c not in live:
+                live["cwq%d" % c] = rot.tile([P, 1024], U32, tag="cw_codes", bufs=5, align_bytes=64, name="cwq%d" % c)
+                live["cws%d" % c] = rot.tile([P, 1024], U8, tag="cw_scales", bufs=5, align_bytes=64, name="cws%d" % c)
+            nc.vector.quantize_mx(
+                out=live["cwq%d" % c][:, h * 512 : (h + 1) * 512].bitcast(FP8X4),
+                scales=live["cws%d" % c][:, h * 512 : (h + 1) * 512],
+                in_=live["cwg%d%d" % (c, h)][:],
+            )
+
+        def combine_passes(c, j, n):
+            acc = psum.tile([P, HALF], F32, tag="acc", name="acc%d%d%d" % (c, j, n))
+            live["acc%d%d%d" % (c, j, n)] = acc
             for g in range(2):
-                sc = slice((2 * j + g) * P, (2 * j + g + 1) * P)
+                rows = slice((2 * j + g) * P, (2 * j + g + 1) * P)
                 nc.tensor.matmul_mx(
                     out=acc[:],
-                    lhsT=t["cwq%d" % c][:, sc].bitcast(FP8X4),
-                    lhsT_scale=t["cws%d" % c][:, sc],
-                    rhs=fq[:, g, n * 512 : (n + 1) * 512].bitcast(FP8X4),
-                    rhs_scale=fs[:, g, n * 512 : (n + 1) * 512],
+                    lhsT=live["cwq%d" % c][:, rows].bitcast(FP8X4),
+                    lhsT_scale=live["cws%d" % c][:, rows],
+                    rhs=f_codes[:, g, n * HALF : (n + 1) * HALF].bitcast(FP8X4),
+                    rhs_scale=f_scales[:, g, n * HALF : (n + 1) * HALF],
                     start=(g == 0),
                     stop=(g == 1),
                 )
 
-        def op_O(c, j, n, eng):
-            acc = t["acc%d%d%d" % (c, j, n)]
-            if c < KE:
-                key = "o%dn%d" % (c, n)
-                if key not in t:
-                    big(key, [P, 4, 512], F32)
-                copy_on(eng, t[key][:, j, :], acc[:])
-            elif c in FINE:
-                key = "o%dj%d" % (c, j)
-                if key not in t:
-                    big(key, [P, D_OUT], F32)
-                copy_on(eng, t[key][:, n * 512 : (n + 1) * 512], acc[:])
-            else:
-                key = "o%dh%d" % (c, j // 2)
-                if key not in t:
-                    big(key, [P, 2, D_OUT], F32)
-                copy_on(eng, t[key][:, j % 2, n * 512 : (n + 1) * 512], acc[:])
+        def half_rows(c, n, engines):
+            for j in range(4):
+                combine_passes(c, j, n)
+            o_tile = big_tile("o%dn%d" % (c, n), [P, 4, HALF], F32)
+            for j in range(4):
+                copy_on(engines[j], o_tile[:, j, :], live["acc%d%d%d" % (c, j, n)][:])
+            nc.sync.dma_start(out=out_rows[c][:, :, n * HALF : (n + 1) * HALF], in_=o_tile[:])
 
-        def op_st(c, x):
-            if c < KE:
-                nc.sync.dma_start(out=out_rows[c][:, :, x * 512 : (x + 1) * 512], in_=t["o%dn%d" % (c, x)][:])
-            elif c in FINE:
-                nc.sync.dma_start(out=out_rows[c][:, x, :], in_=t["o%dj%d" % (c, x)][:])
-            else:
-                nc.sync.dma_start(out=out_rows[c][:, 2 * x : 2 * x + 2, :], in_=t["o%dh%d" % (c, x)][:])
+        def whole_rows(c, tiles_a_store, quantise_next):
+            for j in range(4):
+                if j % tiles_a_store == 0:
+                    o_tile = big_tile("o%dj%d" % (c, j), [P, tiles_a_store, D_OUT], F32)
+                for n in range(2):
+                    combine_passes(c, j, n)
+                    copy_on("vs"[n], o_tile[:, j % tiles_a_store, n * HALF : (n + 1) * HALF], live["acc%d%d%d" % (c, j, n)][:])
+                if (j + 1) % tiles_a_store == 0:
+                    nc.sync.dma_start(out=out_rows[c][:, j + 1 - tiles_a_store : j + 1, :], in_=o_tile[:])
+                if quantise_next and j < 2:
+                    quantise_cw(c + 1, j)
 
-        ops = {
-            "ms": op_ms, "id": op_id, "lb": op_lb, "lx": op_lx, "lw": op_lw, "lc": op_lc, "bm": op_bm, "bc": op_bc,
-            "xT": op_xT, "xc": op_xc, "qx": op_qx, "R": op_R, "qW": op_qW, "S1": op_S1, "B": op_B, "qF": op_qF,
-            "T": op_T, "Tc": op_Tc, "qC": op_qC, "MM": op_MM, "O": op_O, "st": op_st,
-        }
-        for step in ORDER:
-            ops[step[0]](*step[1:])
+        zero_bias_row()
+        make_identity(nc, ident[:])
+        load_x(0)
+        load_x(1)
+        load_w(0)
+        load_bias()
+        for a in range(1, EXPERTS):
+            load_w(a)
+        for c in range(SUPER_TILES):
+            load_cw(c)
+
+        transpose_x()
+        copy_x("svsv")
+        spread_bias()
+        copy_bias()
+
+        quantise_x(0)
+        regroup_w(0, 0, "v")
+        regroup_w(0, 1, "v")
+        regroup_w(1, 1, "v")
+        regroup_w(1, 0, "s")
+        regroup_w(2, 0, "s")
+        regroup_w(3, 0, "s")
+        regroup_w(2, 1, "s")
+        quantise_w(0, 0)
+        quantise_x(1)
+        quantise_w(1, 0)
+        quantise_w(0, 1)
+        quantise_w(1, 1)
+
+        stage1_passes(0, 0)
+        stage1_bias(0, 0)
+        quantise_w(2, 0)
+        quantise_w(3, 0)
+        quantise_flat(0, 0)
+        transpose_cw(0)
+        copy_cw(0, "ssss")
+        stage1_passes(1, 0)
+        stage1_bias(1, 0)
+        quantise_cw(0, 0)
+        quantise_cw(0, 1)
+        quantise_flat(1, 0)
+        regroup_w(3, 1, "v")
+        quantise_w(3, 1)
+        transpose_cw(1)
+        copy_cw(1, "ssss")
+        transpose_cw(2)
+        copy_cw(2, "svvs")
+
+        half_rows(0, 0, "ssss")
+        stage1_passes(0, 1)
+        quantise_cw(1, 0)
+        quantise_cw(1, 1)
+        quantise_w(2, 1)
+        stage1_bias(0, 1)
+        transpose_cw(3)
+        copy_cw(3, "ssvs")
+        half_rows(1, 0, "ssss")
+        quantise_cw(2, 0)
+        quantise_cw(2, 1)
+        quantise_flat(0, 1)
+        transpose_cw(4)
+        copy_cw(4, "svss")
+        half_rows(2, 0, "vvss")
+        quantise_cw(3, 0)
+        quantise_cw(3, 1)
+        stage1_passes(1, 1)
+        stage1_bias(1, 1)
+        quantise_flat(1, 1)
+        transpose_cw(5)
+        copy_cw(5, "ssvv")
+        quantise_cw(4, 0)
+        quantise_cw(4, 1)
+        half_rows(3, 0, "ssss")
+
+        for c in range(EARLY):
+            half_rows(c, 1, "ssvs")
+            if c == 1:
+                quantise_cw(5, 0)
+                quantise_cw(5, 1)
+
+        for c in range(EARLY, SUPER_TILES):
+            prepare_next = EARLY + 1 < c + 1 < SUPER_TILES
+            if prepare_next:
+                transpose_cw(c + 1)
+                copy_cw(c + 1, "svss")
+            whole_rows(c, 2 if c < SUPER_TILES - 2 else 1, prepare_next)

@@ -221,8 +221,8 @@ def tile_expertparallelbehindblock_t_kernel(tc, inputs, combine_weights, weight,
                 copy_on(engines[j], o_tile[:, j, :], live["acc%d%d%d" % (c, j, n)][:])
             nc.sync.dma_start(out=out_rows[c][:, :, n * HALF : (n + 1) * HALF], in_=o_tile[:])
 
-        def whole_rows(c, tiles_a_store, quantise_next):
-            for j in range(4):
+        def whole_rows(c, tiles_a_store, quantise_next, tiles=4):
+            for j in range(tiles):
                 if j % tiles_a_store == 0:
                     o_tile = big_tile("o%dj%d" % (c, j), [P, tiles_a_store, D_OUT], F32)
                 for n in range(2):
@@ -232,6 +232,25 @@ def tile_expertparallelbehindblock_t_kernel(tc, inputs, combine_weights, weight,
                     nc.sync.dma_start(out=out_rows[c][:, j + 1 - tiles_a_store : j + 1, :], in_=o_tile[:])
                 if quantise_next and j < 2:
                     quantise_cw(c + 1, j)
+
+        def last_tile(c, j):
+            o_tile = big_tile("o_last", [P, D_OUT], F32)
+            for q in range(4):
+                cols = slice(q * 256, (q + 1) * 256)
+                acc = psum.tile([P, 256], F32, tag="acc", name="acc_last%d" % q)
+                for g in range(2):
+                    rows = slice((2 * j + g) * P, (2 * j + g + 1) * P)
+                    nc.tensor.matmul_mx(
+                        out=acc[:],
+                        lhsT=live["cwq%d" % c][:, rows].bitcast(FP8X4),
+                        lhsT_scale=live["cws%d" % c][:, rows],
+                        rhs=f_codes[:, g, cols].bitcast(FP8X4),
+                        rhs_scale=f_scales[:, g, cols],
+                        start=(g == 0),
+                        stop=(g == 1),
+                    )
+                copy_on("vs"[q % 2], o_tile[:, cols], acc[:])
+                nc.sync.dma_start(out=out_rows[c][:, j, cols], in_=o_tile[:, cols])
 
         zero_bias_row()
         make_identity(nc, ident[:])
@@ -319,4 +338,8 @@ def tile_expertparallelbehindblock_t_kernel(tc, inputs, combine_weights, weight,
             if prepare_next:
                 transpose_cw(c + 1)
                 copy_cw(c + 1, "svss")
-            whole_rows(c, 2 if c < SUPER_TILES - 2 else 1, prepare_next)
+            if c < SUPER_TILES - 1:
+                whole_rows(c, 2 if c < SUPER_TILES - 2 else 1, prepare_next)
+            else:
+                whole_rows(c, 1, False, tiles=3)
+                last_tile(c, 3)

@@ -15,9 +15,9 @@ P = 128
 EXPERTS = 4
 D_IN = 512
 D_OUT = 1024
+QUARTER = 256
 HALF = 512
 SUPER_TILES = 8
-EARLY = 4
 FLOPS = 2 * 1024 * D_IN * D_OUT + 2 * 4096 * 1024 * D_OUT
 
 
@@ -62,15 +62,17 @@ def tile_expertparallelbehindblock_t_kernel(tc, inputs, combine_weights, weight,
                 in_=inputs[512 * h : 512 * (h + 1), :].rearrange("(a p e) k -> p a e k", a=2, e=2),
             )
 
-        def load_w(a):
-            raw = big_tile("w%d" % a, [P, 4, D_OUT], BF16)
+        def load_w(a, n):
+            if n == 0:
+                big_tile("w%d" % a, [P, 4, D_OUT], BF16)
+            cols = slice(n * HALF, (n + 1) * HALF)
             nc.sync.dma_start(
-                out=raw[:].rearrange("p (u e) d -> p u e d", e=2),
-                in_=weight[a].rearrange("(u q e) d -> q u e d", u=2, e=2),
+                out=live["w%d" % a][:, :, cols],
+                in_=weight[a][:, cols].rearrange("(q t) d -> q t d", t=4),
             )
 
         def load_cw(c):
-            live["cw%d" % c] = rot.tile([P, 4, 1024], BF16, tag="cw", bufs=6, name="cw%d" % c)
+            live["cw%d" % c] = rot.tile([P, 4, 1024], BF16, tag="cw", bufs=5, name="cw%d" % c)
             nc.sync.dma_start(out=live["cw%d" % c][:], in_=cw_rows[c])
 
         def zero_bias_row():
@@ -81,19 +83,17 @@ def tile_expertparallelbehindblock_t_kernel(tc, inputs, combine_weights, weight,
         def load_bias():
             nc.sync.dma_start(out=live["bias_row"][0:1, :], in_=bias.rearrange("e o d -> o (e d)"))
 
-        def spread_bias():
-            for a in range(EXPERTS):
-                bank = psum.tile([P, D_OUT], BF16, tag="acc", name="bias_ps%d" % a)
-                live["bias_ps%d" % a] = bank
-                for h in range(2):
-                    cols = slice(a * D_OUT + h * HALF, a * D_OUT + (h + 1) * HALF)
-                    nc.tensor.matmul(
-                        bank[:, h * HALF : (h + 1) * HALF], lhsT=ones[:], rhs=live["bias_row"][:, cols], start=True, stop=True
-                    )
+        def spread_bias(n):
+            for b in range(2):
+                bank = psum.tile([P, 2, HALF], BF16, tag="acc", name="bias_ps%d%d" % (n, b))
+                live["bias_ps%d%d" % (n, b)] = bank
+                for i in range(2):
+                    first = (2 * b + i) * D_OUT + n * HALF
+                    nc.tensor.matmul(bank[:, i, :], lhsT=ones[:], rhs=live["bias_row"][:, first : first + HALF], start=True, stop=True)
 
-        def copy_bias():
-            for a in range(EXPERTS):
-                nc.scalar.copy(out=bias_all[:, a, :], in_=live["bias_ps%d" % a][:])
+        def copy_bias(n):
+            for b in range(2):
+                nc.scalar.copy(out=bias_all[:, 2 * b : 2 * b + 2, n * HALF : (n + 1) * HALF], in_=live["bias_ps%d%d" % (n, b)][:])
 
         def transpose_x():
             words = live["x"][:].bitcast(F32)
@@ -102,10 +102,9 @@ def tile_expertparallelbehindblock_t_kernel(tc, inputs, combine_weights, weight,
                 live["x_ps%d" % i] = bank
                 for i2 in range(2):
                     for u in range(2):
-                        nc.tensor.transpose(bank[:, i2, u, :], words[:, 2 * i + i2, u * P : (u + 1) * P], ident[:])
+                        nc.tensor.transpose(bank[:, i2, u, :], words[:, 2 * i + i2, u : D_IN // 2 : 2], ident[:])
 
         def copy_x(engines):
-            big_tile("x_grouped", [P, 4096], BF16)
             words = live["x_grouped"][:].bitcast(F32).rearrange("p (i s u) -> p i s u", i=8, u=2)
             for i in range(4):
                 copy_on(engines[i], words[:, 2 * i : 2 * i + 2, :, :], live["x_ps%d" % i][:].rearrange("p i u s -> p i s u"))
@@ -117,23 +116,23 @@ def tile_expertparallelbehindblock_t_kernel(tc, inputs, combine_weights, weight,
                 in_=live["x_grouped"][:, g * 2048 : (g + 1) * 2048],
             )
 
-        def regroup_w(a, n, engine):
-            grouped = rot.tile([P, 4 * HALF], BF16, tag="w_grouped", bufs=6, align_bytes=64, name="wg%d%d" % (a, n))
-            live["wg%d%d" % (a, n)] = grouped
+        def regroup_w(a, lo, width, engine):
+            grouped = rot.tile([P, 4 * width], BF16, tag="w_grouped%d" % width, bufs=4 if width == 256 else 2, align_bytes=64, name="wg%d_%d" % (a, lo))
+            live["wg%d_%d" % (a, lo)] = grouped
             copy_on(
                 engine,
                 grouped[:].rearrange("p (c i t) -> p c t i", i=4, t=4),
-                live["w%d" % a][:, :, n * HALF : (n + 1) * HALF].rearrange("p t (c i) -> p c t i", i=4),
+                live["w%d" % a][:, :, lo : lo + width].rearrange("p t (c i) -> p c t i", i=4),
             )
 
-        def quantise_w(a, n):
-            cols = slice(n * HALF, (n + 1) * HALF)
+        def quantise_w(a, lo, width):
+            cols = slice(lo, lo + width)
             nc.vector.quantize_mx(
-                out=w_codes[:, a, cols].bitcast(FP8X4), scales=w_scales[:, a, cols], in_=live["wg%d%d" % (a, n)][:]
+                out=w_codes[:, a, cols].bitcast(FP8X4), scales=w_scales[:, a, cols], in_=live["wg%d_%d" % (a, lo)][:]
             )
 
-        def stage1_passes(g, n):
-            for d in range(4 * n, 4 * n + 4):
+        def stage1_passes(g, lo, width):
+            for d in range(lo // P, (lo + width) // P):
                 cols = slice(d * P, (d + 1) * P)
                 bank = psum.tile([P, 2, 2, P], F32, tag="acc", name="f_ps%d%d" % (g, d))
                 live["f_ps%d%d" % (g, d)] = bank
@@ -151,25 +150,25 @@ def tile_expertparallelbehindblock_t_kernel(tc, inputs, combine_weights, weight,
                             stop=True,
                         )
 
-        def stage1_bias(g, n):
-            grouped = rot.tile([P, HALF, 4], BF16, tag="f_grouped", bufs=4, align_bytes=64, name="fg%d%d" % (g, n))
-            live["fg%d%d" % (g, n)] = grouped
-            for d in range(4 * n, 4 * n + 4):
-                cols = slice(d * P, (d + 1) * P)
-                b_view = bias_all[:, 2 * g : 2 * g + 2, cols].rearrange("p u d -> p d u").unsqueeze(3)
+        def stage1_bias(g, lo, width):
+            grouped = rot.tile([P, width, 4], BF16, tag="f_grouped%d" % width, bufs=2, align_bytes=64, name="fg%d_%d" % (g, lo))
+            live["fg%d_%d" % (g, lo)] = grouped
+            for i in range(width // P):
+                d = lo // P + i
+                b_view = bias_all[:, 2 * g : 2 * g + 2, d * P : (d + 1) * P].rearrange("p u d -> p d u").unsqueeze(3)
                 nc.vector.tensor_tensor(
-                    out=grouped[:, (d - 4 * n) * P : (d - 4 * n + 1) * P, :].rearrange("p d (u e) -> p d u e", e=2),
+                    out=grouped[:, i * P : (i + 1) * P, :].rearrange("p d (u e) -> p d u e", e=2),
                     in0=live["f_ps%d%d" % (g, d)][:].rearrange("p u e d -> p d u e"),
                     in1=b_view.to_broadcast([P, P, 2, 2]),
                     op=ADD,
                 )
 
-        def quantise_flat(g, n):
-            cols = slice(n * HALF, (n + 1) * HALF)
+        def quantise_flat(g, lo, width):
+            cols = slice(lo, lo + width)
             nc.vector.quantize_mx(
                 out=f_codes[:, g, cols].bitcast(FP8X4),
                 scales=f_scales[:, g, cols],
-                in_=live["fg%d%d" % (g, n)][:].rearrange("p d t -> p (d t)"),
+                in_=live["fg%d_%d" % (g, lo)][:].rearrange("p d t -> p (d t)"),
             )
 
         def transpose_cw(c):
@@ -184,162 +183,164 @@ def tile_expertparallelbehindblock_t_kernel(tc, inputs, combine_weights, weight,
             for j in range(4):
                 key = "cwg%d%d" % (c, j // 2)
                 if key not in live:
-                    live[key] = rot.tile([P, 2048], BF16, tag="cw_grouped", bufs=5, align_bytes=64, name=key)
+                    live[key] = rot.tile([P, 2048], BF16, tag="cw_grouped", bufs=4, align_bytes=64, name=key)
                 words = live[key][:].bitcast(F32).rearrange("p (j g s u) -> p j g s u", j=2, g=2, u=2)
                 copy_on(engines[j], words[:, j % 2], live["cw_ps%d%d" % (c, j)][:].rearrange("p (g u) s -> p g s u", u=2))
 
         def quantise_cw(c, h):
             if "cwq%d" % c not in live:
-                live["cwq%d" % c] = rot.tile([P, 1024], U32, tag="cw_codes", bufs=5, align_bytes=64, name="cwq%d" % c)
-                live["cws%d" % c] = rot.tile([P, 1024], U8, tag="cw_scales", bufs=5, align_bytes=64, name="cws%d" % c)
+                live["cwq%d" % c] = rot.tile([P, 1024], U32, tag="cw_codes", bufs=8, align_bytes=64, name="cwq%d" % c)
+                live["cws%d" % c] = rot.tile([P, 1024], U8, tag="cw_scales", bufs=8, align_bytes=64, name="cws%d" % c)
             nc.vector.quantize_mx(
                 out=live["cwq%d" % c][:, h * 512 : (h + 1) * 512].bitcast(FP8X4),
                 scales=live["cws%d" % c][:, h * 512 : (h + 1) * 512],
                 in_=live["cwg%d%d" % (c, h)][:],
             )
 
-        def combine_passes(c, j, n):
-            acc = psum.tile([P, HALF], F32, tag="acc", name="acc%d%d%d" % (c, j, n))
-            live["acc%d%d%d" % (c, j, n)] = acc
+        def combine_passes(acc, c, j, lo, width):
             for g in range(2):
                 rows = slice((2 * j + g) * P, (2 * j + g + 1) * P)
                 nc.tensor.matmul_mx(
-                    out=acc[:],
+                    out=acc,
                     lhsT=live["cwq%d" % c][:, rows].bitcast(FP8X4),
                     lhsT_scale=live["cws%d" % c][:, rows],
-                    rhs=f_codes[:, g, n * HALF : (n + 1) * HALF].bitcast(FP8X4),
-                    rhs_scale=f_scales[:, g, n * HALF : (n + 1) * HALF],
+                    rhs=f_codes[:, g, lo : lo + width].bitcast(FP8X4),
+                    rhs_scale=f_scales[:, g, lo : lo + width],
                     start=(g == 0),
                     stop=(g == 1),
                 )
 
-        def half_rows(c, n, engines):
-            for j in range(4):
-                combine_passes(c, j, n)
+        def quarter_rows(c, q, engines):
+            n = q // 2
+            if q % 2 == 0:
+                big_tile("o%dn%d" % (c, n), [P, 4, HALF], F32)
+            o_tile = live["o%dn%d" % (c, n)]
+            for i in range(2):
+                bank = psum.tile([P, 2, QUARTER], F32, tag="acc", name="acc%dq%d%d" % (c, q, i))
+                for j in range(2):
+                    combine_passes(bank[:, j, :], c, 2 * i + j, q * QUARTER, QUARTER)
+                copy_on(engines[i], o_tile[:, 2 * i : 2 * i + 2, (q % 2) * QUARTER : (q % 2 + 1) * QUARTER], bank[:])
+            if q % 2 == 1:
+                nc.sync.dma_start(out=out_rows[c][:, :, n * HALF : (n + 1) * HALF], in_=o_tile[:])
+
+        def half_rows(c, n, engines, parts=1):
             o_tile = big_tile("o%dn%d" % (c, n), [P, 4, HALF], F32)
+            each = 4 // parts
             for j in range(4):
-                copy_on(engines[j], o_tile[:, j, :], live["acc%d%d%d" % (c, j, n)][:])
-            nc.sync.dma_start(out=out_rows[c][:, :, n * HALF : (n + 1) * HALF], in_=o_tile[:])
-
-        def whole_rows(c, tiles_a_store, quantise_next, tiles=4):
-            for j in range(tiles):
-                if j % tiles_a_store == 0:
-                    o_tile = big_tile("o%dj%d" % (c, j), [P, tiles_a_store, D_OUT], F32)
-                for n in range(2):
-                    combine_passes(c, j, n)
-                    copy_on("vs"[n], o_tile[:, j % tiles_a_store, n * HALF : (n + 1) * HALF], live["acc%d%d%d" % (c, j, n)][:])
-                if (j + 1) % tiles_a_store == 0:
-                    nc.sync.dma_start(out=out_rows[c][:, j + 1 - tiles_a_store : j + 1, :], in_=o_tile[:])
-                if quantise_next and j < 2:
-                    quantise_cw(c + 1, j)
-
-        def last_tile(c, j):
-            o_tile = big_tile("o_last", [P, D_OUT], F32)
-            for q in range(4):
-                cols = slice(q * 256, (q + 1) * 256)
-                acc = psum.tile([P, 256], F32, tag="acc", name="acc_last%d" % q)
-                for g in range(2):
-                    rows = slice((2 * j + g) * P, (2 * j + g + 1) * P)
-                    nc.tensor.matmul_mx(
-                        out=acc[:],
-                        lhsT=live["cwq%d" % c][:, rows].bitcast(FP8X4),
-                        lhsT_scale=live["cws%d" % c][:, rows],
-                        rhs=f_codes[:, g, cols].bitcast(FP8X4),
-                        rhs_scale=f_scales[:, g, cols],
-                        start=(g == 0),
-                        stop=(g == 1),
-                    )
-                copy_on("vs"[q % 2], o_tile[:, cols], acc[:])
-                nc.sync.dma_start(out=out_rows[c][:, j, cols], in_=o_tile[:, cols])
+                acc = psum.tile([P, HALF], F32, tag="acc", name="acc%d%d%d" % (c, j, n))
+                combine_passes(acc[:], c, j, n * HALF, HALF)
+                copy_on(engines[j], o_tile[:, j, :], acc[:])
+                if (j + 1) % each == 0:
+                    rows = slice(j + 1 - each, j + 1)
+                    nc.sync.dma_start(out=out_rows[c][:, rows, n * HALF : (n + 1) * HALF], in_=o_tile[:, rows, :])
 
         zero_bias_row()
         make_identity(nc, ident[:])
         load_x(0)
         load_x(1)
-        load_w(0)
+        big_tile("x_grouped", [P, 4096], BF16)
+        load_w(0, 0)
         load_bias()
-        for a in range(1, EXPERTS):
-            load_w(a)
-        for c in range(SUPER_TILES):
+        load_w(1, 0)
+        load_cw(0)
+        load_w(2, 0)
+        load_w(3, 0)
+        for c in range(1, 5):
             load_cw(c)
+        for a in range(EXPERTS):
+            load_w(a, 1)
+        load_cw(5)
 
         transpose_x()
-        copy_x("svsv")
-        spread_bias()
-        copy_bias()
-
+        copy_x("svss")
         quantise_x(0)
-        regroup_w(0, 0, "v")
-        regroup_w(0, 1, "v")
-        regroup_w(1, 1, "v")
-        regroup_w(1, 0, "s")
-        regroup_w(2, 0, "s")
-        regroup_w(3, 0, "s")
-        regroup_w(2, 1, "s")
-        quantise_w(0, 0)
+        spread_bias(0)
+        copy_bias(0)
+        regroup_w(0, 0, 256, "v")
         quantise_x(1)
-        quantise_w(1, 0)
-        quantise_w(0, 1)
-        quantise_w(1, 1)
-
-        stage1_passes(0, 0)
-        stage1_bias(0, 0)
-        quantise_w(2, 0)
-        quantise_w(3, 0)
-        quantise_flat(0, 0)
+        quantise_w(0, 0, 256)
+        regroup_w(1, 0, 256, "v")
+        spread_bias(1)
+        copy_bias(1)
+        quantise_w(1, 0, 256)
+        stage1_passes(0, 0, 256)
         transpose_cw(0)
         copy_cw(0, "ssss")
-        stage1_passes(1, 0)
-        stage1_bias(1, 0)
+        stage1_bias(0, 0, 256)
+        regroup_w(2, 0, 256, "v")
+        regroup_w(3, 0, 256, "v")
+        quantise_w(2, 0, 256)
+        quantise_w(3, 0, 256)
+        stage1_passes(1, 0, 256)
+        regroup_w(0, 256, 256, "s")
+        quantise_flat(0, 0, 256)
         quantise_cw(0, 0)
-        quantise_cw(0, 1)
-        quantise_flat(1, 0)
-        regroup_w(3, 1, "v")
-        quantise_w(3, 1)
+        stage1_bias(1, 0, 256)
         transpose_cw(1)
+        regroup_w(1, 256, 256, "s")
+        quantise_cw(0, 1)
+        quantise_flat(1, 0, 256)
         copy_cw(1, "ssss")
+        quarter_rows(0, 0, "ss")
+        regroup_w(2, 256, 256, "v")
+        quantise_w(0, 256, 256)
+        quantise_w(1, 256, 256)
+        regroup_w(3, 256, 256, "v")
+        stage1_passes(0, 256, 256)
         transpose_cw(2)
-        copy_cw(2, "svvs")
-
-        half_rows(0, 0, "ssss")
-        stage1_passes(0, 1)
+        quantise_w(2, 256, 256)
         quantise_cw(1, 0)
         quantise_cw(1, 1)
-        quantise_w(2, 1)
-        stage1_bias(0, 1)
+        stage1_bias(0, 256, 256)
+        quantise_w(3, 256, 256)
+        copy_cw(2, "ssss")
+        quarter_rows(1, 0, "ss")
+        stage1_passes(1, 256, 256)
         transpose_cw(3)
-        copy_cw(3, "ssvs")
-        half_rows(1, 0, "ssss")
+        quantise_flat(0, 256, 256)
+        stage1_bias(1, 256, 256)
         quantise_cw(2, 0)
         quantise_cw(2, 1)
-        quantise_flat(0, 1)
+        quantise_flat(1, 256, 256)
+        copy_cw(3, "ssss")
+        load_cw(6)
+        load_cw(7)
+        quarter_rows(2, 0, "ss")
+        regroup_w(0, 512, 512, "v")
+        quarter_rows(0, 1, "ss")
         transpose_cw(4)
-        copy_cw(4, "svss")
-        half_rows(2, 0, "vvss")
         quantise_cw(3, 0)
         quantise_cw(3, 1)
-        stage1_passes(1, 1)
-        stage1_bias(1, 1)
-        quantise_flat(1, 1)
-        transpose_cw(5)
-        copy_cw(5, "ssvv")
-        quantise_cw(4, 0)
-        quantise_cw(4, 1)
-        half_rows(3, 0, "ssss")
+        quarter_rows(1, 1, "ss")
+        copy_cw(4, "sssv")
+        regroup_w(1, 512, 512, "v")
+        quarter_rows(2, 1, "ss")
+        quantise_w(0, 512, 512)
 
-        for c in range(EARLY):
-            half_rows(c, 1, "ssvs")
-            if c == 1:
-                quantise_cw(5, 0)
-                quantise_cw(5, 1)
+        for c in range(3, 7):
+            if c + 2 < SUPER_TILES:
+                transpose_cw(c + 2)
+            if c == 3:
+                quantise_w(1, 512, 512)
+                regroup_w(2, 512, 512, "v")
+                regroup_w(3, 512, 512, "v")
+            elif c == 4:
+                stage1_passes(0, 512, 512)
+                stage1_bias(0, 512, 512)
+                quantise_w(2, 512, 512)
+                quantise_w(3, 512, 512)
+            elif c == 5:
+                stage1_passes(1, 512, 512)
+                quantise_flat(0, 512, 512)
+                stage1_bias(1, 512, 512)
+                quantise_flat(1, 512, 512)
+            quantise_cw(c + 1, 0)
+            quantise_cw(c + 1, 1)
+            if c + 2 < SUPER_TILES:
+                copy_cw(c + 2, "ssss")
+            half_rows(c, 0, "vsvs" if c == 6 else "ssss")
 
-        for c in range(EARLY, SUPER_TILES):
-            prepare_next = EARLY + 1 < c + 1 < SUPER_TILES
-            if prepare_next:
-                transpose_cw(c + 1)
-                copy_cw(c + 1, "svss")
-            if c < SUPER_TILES - 1:
-                whole_rows(c, 2 if c < SUPER_TILES - 2 else 1, prepare_next)
-            else:
-                whole_rows(c, 1, False, tiles=3)
-                last_tile(c, 3)
+        for c in range(7):
+            half_rows(c, 1, "vsvs")
+        half_rows(7, 0, "vsvs", 2)
+        half_rows(7, 1, "vsvs", 4)

@@ -34,7 +34,7 @@ def tile_expertparallelbehindblock_t_kernel(tc, inputs, combine_weights, weight,
 
         ident = keep.tile([P, P], F32)
         ones = keep.tile([P, P], BF16)
-        bias_all = keep.tile([P, EXPERTS, D_OUT], BF16)
+        bias_all = keep.tile([P, 2, EXPERTS, HALF], BF16)
         x_codes = keep.tile([P, 8 * P], U32, align_bytes=64)
         x_scales = keep.tile([P, 8 * P], U8, align_bytes=64)
         w_codes = keep.tile([P, EXPERTS, D_OUT], U32, align_bytes=64)
@@ -45,7 +45,7 @@ def tile_expertparallelbehindblock_t_kernel(tc, inputs, combine_weights, weight,
         live = {}
 
         def big_tile(name, shape, dtype):
-            live[name] = rot.tile(shape, dtype, tag="big", bufs=7, align_bytes=64, name=name)
+            live[name] = rot.tile(shape, dtype, tag="big", bufs=6, align_bytes=64, name=name)
             return live[name]
 
         def copy_on(engine, dst, src):
@@ -63,16 +63,12 @@ def tile_expertparallelbehindblock_t_kernel(tc, inputs, combine_weights, weight,
             )
 
         def load_w(a, n):
-            if n == 0:
-                big_tile("w%d" % a, [P, 4, D_OUT], BF16)
-            cols = slice(n * HALF, (n + 1) * HALF)
-            nc.sync.dma_start(
-                out=live["w%d" % a][:, :, cols],
-                in_=weight[a][:, cols].rearrange("(q t) d -> q t d", t=4),
-            )
+            raw = rot.tile([P, 4, HALF], BF16, tag="w", bufs=6, name="w%d%d" % (a, n))
+            live["w%d%d" % (a, n)] = raw
+            nc.sync.dma_start(out=raw[:], in_=weight[a][:, n * HALF : (n + 1) * HALF].rearrange("(q t) d -> q t d", t=4))
 
         def load_cw(c):
-            live["cw%d" % c] = rot.tile([P, 4, 1024], BF16, tag="cw", bufs=5, name="cw%d" % c)
+            live["cw%d" % c] = rot.tile([P, 4, 1024], BF16, tag="cw", bufs=4, name="cw%d" % c)
             nc.sync.dma_start(out=live["cw%d" % c][:], in_=cw_rows[c])
 
         def zero_bias_row():
@@ -93,7 +89,7 @@ def tile_expertparallelbehindblock_t_kernel(tc, inputs, combine_weights, weight,
 
         def copy_bias(n):
             for b in range(2):
-                nc.scalar.copy(out=bias_all[:, 2 * b : 2 * b + 2, n * HALF : (n + 1) * HALF], in_=live["bias_ps%d%d" % (n, b)][:])
+                nc.scalar.copy(out=bias_all[:, n, 2 * b : 2 * b + 2, :], in_=live["bias_ps%d%d" % (n, b)][:])
 
         def transpose_x():
             words = live["x"][:].bitcast(F32)
@@ -122,7 +118,7 @@ def tile_expertparallelbehindblock_t_kernel(tc, inputs, combine_weights, weight,
             copy_on(
                 engine,
                 grouped[:].rearrange("p (c i t) -> p c t i", i=4, t=4),
-                live["w%d" % a][:, :, lo : lo + width].rearrange("p t (c i) -> p c t i", i=4),
+                live["w%d%d" % (a, lo // HALF)][:, :, lo % HALF : lo % HALF + width].rearrange("p t (c i) -> p c t i", i=4),
             )
 
         def quantise_w(a, lo, width):
@@ -155,7 +151,7 @@ def tile_expertparallelbehindblock_t_kernel(tc, inputs, combine_weights, weight,
             live["fg%d_%d" % (g, lo)] = grouped
             for i in range(width // P):
                 d = lo // P + i
-                b_view = bias_all[:, 2 * g : 2 * g + 2, d * P : (d + 1) * P].rearrange("p u d -> p d u").unsqueeze(3)
+                b_view = bias_all[:, d // 4, 2 * g : 2 * g + 2, d % 4 * P : (d % 4 + 1) * P].rearrange("p u d -> p d u").unsqueeze(3)
                 nc.vector.tensor_tensor(
                     out=grouped[:, i * P : (i + 1) * P, :].rearrange("p d (u e) -> p d u e", e=2),
                     in0=live["f_ps%d%d" % (g, d)][:].rearrange("p u e d -> p d u e"),

@@ -37,8 +37,10 @@ def tile_expertparallelbehindblock_t_kernel(tc, inputs, combine_weights, weight,
         bias_all = keep.tile([P, 2, EXPERTS, HALF], BF16)
         x_codes = keep.tile([P, 8 * P], U32, align_bytes=64)
         x_scales = keep.tile([P, 8 * P], U8, align_bytes=64)
-        w_codes = keep.tile([P, EXPERTS, D_OUT], U32, align_bytes=64)
-        w_scales = keep.tile([P, EXPERTS, D_OUT], U8, align_bytes=64)
+        w_codes, w_scales = {}, {}
+        for lo, width in ((0, QUARTER), (QUARTER, QUARTER), (HALF, HALF)):
+            w_codes[lo] = keep.tile([P, EXPERTS, width], U32, align_bytes=64, name="w_codes%d" % lo)
+            w_scales[lo] = keep.tile([P, EXPERTS, width], U8, align_bytes=64, name="w_scales%d" % lo)
         f_codes = keep.tile([P, 2, D_OUT], U32, align_bytes=64)
         f_scales = keep.tile([P, 2, D_OUT], U8, align_bytes=64)
 
@@ -113,23 +115,26 @@ def tile_expertparallelbehindblock_t_kernel(tc, inputs, combine_weights, weight,
             )
 
         def regroup_w(a, lo, width, engine):
-            grouped = rot.tile([P, 4 * width], BF16, tag="w_grouped%d" % width, bufs=4 if width == 256 else 2, align_bytes=64, name="wg%d_%d" % (a, lo))
-            live["wg%d_%d" % (a, lo)] = grouped
+            pair = "wg%d_%d" % (a // 2, lo)
+            if pair not in live:
+                live[pair] = rot.tile([P, 2, 4 * width], BF16, tag="w_grouped%d" % width, bufs=3 if width == QUARTER else 1, align_bytes=64, name=pair)
             copy_on(
                 engine,
-                grouped[:].rearrange("p (c i t) -> p c t i", i=4, t=4),
+                live[pair][:, a % 2, :].rearrange("p (c i t) -> p c t i", i=4, t=4),
                 live["w%d%d" % (a, lo // HALF)][:, :, lo % HALF : lo % HALF + width].rearrange("p t (c i) -> p c t i", i=4),
             )
 
-        def quantise_w(a, lo, width):
-            cols = slice(lo, lo + width)
+        def quantise_w(g, lo):
+            experts = slice(2 * g, 2 * g + 2)
             nc.vector.quantize_mx(
-                out=w_codes[:, a, cols].bitcast(FP8X4), scales=w_scales[:, a, cols], in_=live["wg%d_%d" % (a, lo)][:]
+                out=w_codes[lo][:, experts, :].rearrange("p a d -> p (a d)").bitcast(FP8X4),
+                scales=w_scales[lo][:, experts, :].rearrange("p a d -> p (a d)"),
+                in_=live["wg%d_%d" % (g, lo)][:].rearrange("p a k -> p (a k)"),
             )
 
         def stage1_passes(g, lo, width):
             for d in range(lo // P, (lo + width) // P):
-                cols = slice(d * P, (d + 1) * P)
+                cols = slice(d * P - lo, (d + 1) * P - lo)
                 bank = psum.tile([P, 2, 2, P], F32, tag="acc", name="f_ps%d%d" % (g, d))
                 live["f_ps%d%d" % (g, d)] = bank
                 for u in range(2):
@@ -140,8 +145,8 @@ def tile_expertparallelbehindblock_t_kernel(tc, inputs, combine_weights, weight,
                             out=bank[:, u, e, :],
                             lhsT=x_codes[:, slots].bitcast(FP8X4),
                             lhsT_scale=x_scales[:, slots],
-                            rhs=w_codes[:, a, cols].bitcast(FP8X4),
-                            rhs_scale=w_scales[:, a, cols],
+                            rhs=w_codes[lo][:, a, cols].bitcast(FP8X4),
+                            rhs_scale=w_scales[lo][:, a, cols],
                             start=True,
                             stop=True,
                         )
@@ -176,21 +181,16 @@ def tile_expertparallelbehindblock_t_kernel(tc, inputs, combine_weights, weight,
                     nc.tensor.transpose(bank[:, a, :], words[:, j, a * P : (a + 1) * P], ident[:])
 
         def copy_cw(c, engines):
+            live["cwg%d" % c] = rot.tile([P, 4096], BF16, tag="cw_grouped", bufs=2, align_bytes=64, name="cwg%d" % c)
+            words = live["cwg%d" % c][:].bitcast(F32).rearrange("p (j g s u) -> p j g s u", j=4, g=2, u=2)
             for j in range(4):
-                key = "cwg%d%d" % (c, j // 2)
-                if key not in live:
-                    live[key] = rot.tile([P, 2048], BF16, tag="cw_grouped", bufs=4, align_bytes=64, name=key)
-                words = live[key][:].bitcast(F32).rearrange("p (j g s u) -> p j g s u", j=2, g=2, u=2)
-                copy_on(engines[j], words[:, j % 2], live["cw_ps%d%d" % (c, j)][:].rearrange("p (g u) s -> p g s u", u=2))
+                copy_on(engines[j], words[:, j], live["cw_ps%d%d" % (c, j)][:].rearrange("p (g u) s -> p g s u", u=2))
 
-        def quantise_cw(c, h):
-            if "cwq%d" % c not in live:
-                live["cwq%d" % c] = rot.tile([P, 1024], U32, tag="cw_codes", bufs=8, align_bytes=64, name="cwq%d" % c)
-                live["cws%d" % c] = rot.tile([P, 1024], U8, tag="cw_scales", bufs=8, align_bytes=64, name="cws%d" % c)
+        def quantise_cw(c):
+            live["cwq%d" % c] = rot.tile([P, 1024], U32, tag="cw_codes", bufs=7, align_bytes=64, name="cwq%d" % c)
+            live["cws%d" % c] = rot.tile([P, 1024], U8, tag="cw_scales", bufs=7, align_bytes=64, name="cws%d" % c)
             nc.vector.quantize_mx(
-                out=live["cwq%d" % c][:, h * 512 : (h + 1) * 512].bitcast(FP8X4),
-                scales=live["cws%d" % c][:, h * 512 : (h + 1) * 512],
-                in_=live["cwg%d%d" % (c, h)][:],
+                out=live["cwq%d" % c][:].bitcast(FP8X4), scales=live["cws%d" % c][:], in_=live["cwg%d" % c][:]
             )
 
         def combine_passes(acc, c, j, lo, width):
@@ -230,113 +230,121 @@ def tile_expertparallelbehindblock_t_kernel(tc, inputs, combine_weights, weight,
                     rows = slice(j + 1 - each, j + 1)
                     nc.sync.dma_start(out=out_rows[c][:, rows, n * HALF : (n + 1) * HALF], in_=o_tile[:, rows, :])
 
+        def whole_rows(c, tiles_a_store, engines="vs"):
+            for j in range(4):
+                if j % tiles_a_store == 0:
+                    o_tile = big_tile("o%dj%d" % (c, j), [P, tiles_a_store, D_OUT], F32)
+                for n in range(2):
+                    acc = psum.tile([P, HALF], F32, tag="acc", name="acc%d%d%d" % (c, j, n))
+                    combine_passes(acc[:], c, j, n * HALF, HALF)
+                    copy_on(engines[n], o_tile[:, j % tiles_a_store, n * HALF : (n + 1) * HALF], acc[:])
+                if (j + 1) % tiles_a_store == 0:
+                    nc.sync.dma_start(out=out_rows[c][:, j + 1 - tiles_a_store : j + 1, :], in_=o_tile[:])
+
         zero_bias_row()
         make_identity(nc, ident[:])
         load_x(0)
         load_x(1)
-        big_tile("x_grouped", [P, 4096], BF16)
-        load_w(0, 0)
         load_bias()
+        load_w(0, 0)
         load_w(1, 0)
         load_cw(0)
         load_w(2, 0)
         load_w(3, 0)
-        for c in range(1, 5):
-            load_cw(c)
-        for a in range(EXPERTS):
-            load_w(a, 1)
+        load_cw(1)
+        load_cw(2)
+        load_cw(3)
+        load_w(0, 1)
+        load_w(1, 1)
+        load_cw(4)
+        load_w(2, 1)
+        load_w(3, 1)
         load_cw(5)
-
-        transpose_x()
-        copy_x("svss")
-        quantise_x(0)
-        spread_bias(0)
-        copy_bias(0)
-        regroup_w(0, 0, 256, "v")
-        quantise_x(1)
-        quantise_w(0, 0, 256)
-        regroup_w(1, 0, 256, "v")
-        spread_bias(1)
-        copy_bias(1)
-        quantise_w(1, 0, 256)
-        stage1_passes(0, 0, 256)
-        transpose_cw(0)
-        copy_cw(0, "ssss")
-        stage1_bias(0, 0, 256)
-        regroup_w(2, 0, 256, "v")
-        regroup_w(3, 0, 256, "v")
-        quantise_w(2, 0, 256)
-        quantise_w(3, 0, 256)
-        stage1_passes(1, 0, 256)
-        regroup_w(0, 256, 256, "s")
-        quantise_flat(0, 0, 256)
-        quantise_cw(0, 0)
-        stage1_bias(1, 0, 256)
-        transpose_cw(1)
-        regroup_w(1, 256, 256, "s")
-        quantise_cw(0, 1)
-        quantise_flat(1, 0, 256)
-        copy_cw(1, "ssss")
-        quarter_rows(0, 0, "ss")
-        regroup_w(2, 256, 256, "v")
-        quantise_w(0, 256, 256)
-        quantise_w(1, 256, 256)
-        regroup_w(3, 256, 256, "v")
-        stage1_passes(0, 256, 256)
-        transpose_cw(2)
-        quantise_w(2, 256, 256)
-        quantise_cw(1, 0)
-        quantise_cw(1, 1)
-        stage1_bias(0, 256, 256)
-        quantise_w(3, 256, 256)
-        copy_cw(2, "ssss")
-        quarter_rows(1, 0, "ss")
-        stage1_passes(1, 256, 256)
-        transpose_cw(3)
-        quantise_flat(0, 256, 256)
-        stage1_bias(1, 256, 256)
-        quantise_cw(2, 0)
-        quantise_cw(2, 1)
-        quantise_flat(1, 256, 256)
-        copy_cw(3, "ssss")
         load_cw(6)
         load_cw(7)
+        big_tile("x_grouped", [P, 4096], BF16)
+        transpose_x()
+        spread_bias(0)
+        copy_x("svss")
+        quantise_x(0)
+        regroup_w(0, 0, 256, "v")
+        quantise_x(1)
+        spread_bias(1)
+        regroup_w(1, 0, 256, "v")
+        copy_bias(0)
+        quantise_w(0, 0)
+        copy_bias(1)
+        stage1_passes(0, 0, 256)
+        transpose_cw(0)
+        stage1_bias(0, 0, 256)
+        quantise_flat(0, 0, 256)
+        regroup_w(2, 0, 256, "v")
+        regroup_w(3, 0, 256, "v")
+        copy_cw(0, "ssss")
+        regroup_w(0, 256, 256, "s")
+        regroup_w(3, 256, 256, "v")
+        regroup_w(2, 256, 256, "s")
+        quantise_w(1, 0)
+        regroup_w(1, 256, 256, "s")
+        quantise_cw(0)
+        stage1_passes(1, 0, 256)
+        stage1_bias(1, 0, 256)
+        transpose_cw(1)
+        quantise_flat(1, 0, 256)
+        copy_cw(1, "sssv")
+        quantise_w(0, 256)
+        quantise_w(1, 256)
+        quarter_rows(0, 0, "ss")
+        transpose_cw(2)
+        quantise_cw(1)
+        stage1_passes(0, 256, 256)
+        copy_cw(2, "ssvs")
+        stage1_bias(0, 256, 256)
+        transpose_cw(3)
+        copy_cw(3, "ssss")
+        stage1_passes(1, 256, 256)
+        quarter_rows(1, 0, "ss")
+        quantise_cw(2)
+        stage1_bias(1, 256, 256)
+        quantise_flat(0, 256, 256)
         quarter_rows(2, 0, "ss")
-        regroup_w(0, 512, 512, "v")
-        quarter_rows(0, 1, "ss")
+        quantise_cw(3)
+        quantise_flat(1, 256, 256)
         transpose_cw(4)
-        quantise_cw(3, 0)
-        quantise_cw(3, 1)
-        quarter_rows(1, 1, "ss")
-        copy_cw(4, "sssv")
+        regroup_w(0, 512, 512, "v")
         regroup_w(1, 512, 512, "v")
+        copy_cw(4, "sssv")
+        quarter_rows(0, 1, "ss")
+        quarter_rows(1, 1, "ss")
         quarter_rows(2, 1, "ss")
-        quantise_w(0, 512, 512)
-
-        for c in range(3, 7):
-            if c + 2 < SUPER_TILES:
-                transpose_cw(c + 2)
-            if c == 3:
-                quantise_w(1, 512, 512)
-                regroup_w(2, 512, 512, "v")
-                regroup_w(3, 512, 512, "v")
-            elif c == 4:
-                stage1_passes(0, 512, 512)
-                stage1_bias(0, 512, 512)
-                quantise_w(2, 512, 512)
-                quantise_w(3, 512, 512)
-            elif c == 5:
-                stage1_passes(1, 512, 512)
-                quantise_flat(0, 512, 512)
-                stage1_bias(1, 512, 512)
-                quantise_flat(1, 512, 512)
-            quantise_cw(c + 1, 0)
-            quantise_cw(c + 1, 1)
-            if c + 2 < SUPER_TILES:
-                copy_cw(c + 2, "ssss")
-            half_rows(c, 0, "vsvs" if c == 6 else "ssss")
-
-        for c in range(7):
-            half_rows(c, 1, "vsvs")
-        half_rows(7, 0, "vsvs", 2)
-        half_rows(7, 1, "vsvs", 4)
+        half_rows(3, 0, "ssss")
+        transpose_cw(5)
+        quantise_cw(4)
+        quantise_w(0, 512)
+        copy_cw(5, "ssss")
+        regroup_w(2, 512, 512, "v")
+        stage1_passes(0, 512, 512)
+        stage1_bias(0, 512, 512)
+        regroup_w(3, 512, 512, "v")
+        half_rows(4, 0, "ssss")
+        quantise_w(1, 512)
+        quantise_cw(5)
+        transpose_cw(6)
+        copy_cw(6, "ssss")
+        stage1_passes(1, 512, 512)
+        quantise_flat(0, 512, 512)
+        stage1_bias(1, 512, 512)
+        transpose_cw(7)
+        quantise_flat(1, 512, 512)
+        half_rows(5, 0, "ssvs")
+        copy_cw(7, "svvs")
+        half_rows(0, 1, "vsvs")
+        quantise_cw(6)
+        half_rows(1, 1, "vsvs")
+        quantise_cw(7)
+        half_rows(2, 1, "vsvs")
+        half_rows(3, 1, "vsvs")
+        half_rows(4, 1, "vsvs")
+        half_rows(5, 1, "vsvs")
+        whole_rows(6, 2)
+        whole_rows(7, 1)

@@ -33,6 +33,7 @@ def tile_expertparallelbehindblock_t_kernel(tc, inputs, combine_weights, weight,
         out_rows = out.rearrange("b (h p j) d -> (b h) p j d", p=P, j=4)
 
         ident = keep.tile([P, P], F32)
+        ident_bf = keep.tile([P, P], BF16)
         ones = keep.tile([P, P], BF16)
         bias_all = keep.tile([P, 2, EXPERTS, HALF], BF16)
         x_codes = keep.tile([P, 8 * P], U32, align_bytes=64)
@@ -123,6 +124,22 @@ def tile_expertparallelbehindblock_t_kernel(tc, inputs, combine_weights, weight,
                 live[pair][:, a % 2, :].rearrange("p (c i t) -> p c t i", i=4, t=4),
                 live["w%d%d" % (a, lo // HALF)][:, :, lo % HALF : lo % HALF + width].rearrange("p t (c i) -> p c t i", i=4),
             )
+
+        def spread_w(a, lo, engine):
+            pair = "wg%d_%d" % (a // 2, lo)
+            if pair not in live:
+                live[pair] = rot.tile([P, 2, 4 * QUARTER], BF16, tag="w_grouped%d" % QUARTER, bufs=3, align_bytes=64, name=pair)
+            bank = psum.tile([P, 4 * QUARTER], BF16, tag="acc", name="w_ps%d_%d" % (a, lo))
+            for i in range(2):
+                first = lo % HALF + i * P
+                nc.tensor.matmul(
+                    bank[:, i * HALF : (i + 1) * HALF],
+                    lhsT=ident_bf[:],
+                    rhs=live["w%d%d" % (a, lo // HALF)][:, :, first : first + P].rearrange("p t c -> p c t"),
+                    start=True,
+                    stop=True,
+                )
+            copy_on(engine, live[pair][:, a % 2, :], bank[:])
 
         def quantise_w(g, lo):
             experts = slice(2 * g, 2 * g + 2)
@@ -243,6 +260,7 @@ def tile_expertparallelbehindblock_t_kernel(tc, inputs, combine_weights, weight,
 
         zero_bias_row()
         make_identity(nc, ident[:])
+        make_identity(nc, ident_bf[:])
         load_x(0)
         load_x(1)
         load_bias()
@@ -264,80 +282,80 @@ def tile_expertparallelbehindblock_t_kernel(tc, inputs, combine_weights, weight,
         load_cw(7)
         big_tile("x_grouped", [P, 4096], BF16)
         transpose_x()
-        spread_bias(0)
-        copy_x("svss")
+        copy_x("svvs")
         quantise_x(0)
-        regroup_w(0, 0, 256, "v")
-        quantise_x(1)
+        spread_bias(0)
         spread_bias(1)
+        regroup_w(0, 0, 256, "v")
         regroup_w(1, 0, 256, "v")
-        copy_bias(0)
         quantise_w(0, 0)
-        copy_bias(1)
         stage1_passes(0, 0, 256)
-        transpose_cw(0)
+        copy_bias(0)
+        copy_bias(1)
+        quantise_x(1)
         stage1_bias(0, 0, 256)
-        quantise_flat(0, 0, 256)
         regroup_w(2, 0, 256, "v")
+        spread_w(0, 256, "s")
+        spread_w(1, 256, "v")
+        transpose_cw(0)
         regroup_w(3, 0, 256, "v")
-        copy_cw(0, "ssss")
-        regroup_w(0, 256, 256, "s")
-        regroup_w(3, 256, 256, "v")
-        regroup_w(2, 256, 256, "s")
         quantise_w(1, 0)
-        regroup_w(1, 256, 256, "s")
+        quantise_flat(0, 0, 256)
+        copy_cw(0, "ssss")
         quantise_cw(0)
+        regroup_w(3, 256, 256, "s")
         stage1_passes(1, 0, 256)
-        stage1_bias(1, 0, 256)
         transpose_cw(1)
+        stage1_bias(1, 0, 256)
         quantise_flat(1, 0, 256)
         copy_cw(1, "sssv")
-        quantise_w(0, 256)
-        quantise_w(1, 256)
+        spread_w(2, 256, "s")
         quarter_rows(0, 0, "ss")
-        transpose_cw(2)
+        quantise_w(0, 256)
         quantise_cw(1)
+        transpose_cw(2)
+        quantise_w(1, 256)
         stage1_passes(0, 256, 256)
-        copy_cw(2, "ssvs")
         stage1_bias(0, 256, 256)
+        copy_cw(2, "ssss")
         transpose_cw(3)
-        copy_cw(3, "ssss")
-        stage1_passes(1, 256, 256)
-        quarter_rows(1, 0, "ss")
         quantise_cw(2)
+        stage1_passes(1, 256, 256)
+        copy_cw(3, "ssss")
         stage1_bias(1, 256, 256)
-        quantise_flat(0, 256, 256)
+        quarter_rows(1, 0, "ss")
         quarter_rows(2, 0, "ss")
-        quantise_cw(3)
-        quantise_flat(1, 256, 256)
         transpose_cw(4)
+        quantise_flat(0, 256, 256)
+        quantise_flat(1, 256, 256)
         regroup_w(0, 512, 512, "v")
         regroup_w(1, 512, 512, "v")
+        quantise_cw(3)
         copy_cw(4, "sssv")
         quarter_rows(0, 1, "ss")
         quarter_rows(1, 1, "ss")
-        quarter_rows(2, 1, "ss")
+        quantise_w(0, 512)
+        quantise_cw(4)
         half_rows(3, 0, "ssss")
         transpose_cw(5)
-        quantise_cw(4)
-        quantise_w(0, 512)
         copy_cw(5, "ssss")
         regroup_w(2, 512, 512, "v")
         stage1_passes(0, 512, 512)
+        half_rows(4, 0, "ssss")
+        quarter_rows(2, 1, "ss")
+        transpose_cw(6)
         stage1_bias(0, 512, 512)
         regroup_w(3, 512, 512, "v")
-        half_rows(4, 0, "ssss")
         quantise_w(1, 512)
         quantise_cw(5)
-        transpose_cw(6)
-        copy_cw(6, "ssss")
+        copy_cw(6, "sssv")
         stage1_passes(1, 512, 512)
         quantise_flat(0, 512, 512)
         stage1_bias(1, 512, 512)
-        transpose_cw(7)
         quantise_flat(1, 512, 512)
+        transpose_cw(7)
         half_rows(5, 0, "ssvs")
-        copy_cw(7, "svvs")
+        copy_cw(7, "vsvs")
         half_rows(0, 1, "vsvs")
         quantise_cw(6)
         half_rows(1, 1, "vsvs")

@@ -33,7 +33,6 @@ def tile_expertparallelbehindblock_t_kernel(tc, inputs, combine_weights, weight,
         out_rows = out.rearrange("b (h p j) d -> (b h) p j d", p=P, j=4)
 
         ident = keep.tile([P, P], F32)
-        ident_bf = keep.tile([P, P], BF16)
         ones = keep.tile([P, P], BF16)
         bias_all = keep.tile([P, 2, EXPERTS, HALF], BF16)
         x_codes = keep.tile([P, 8 * P], U32, align_bytes=64)
@@ -124,22 +123,6 @@ def tile_expertparallelbehindblock_t_kernel(tc, inputs, combine_weights, weight,
                 live[pair][:, a % 2, :].rearrange("p (c i t) -> p c t i", i=4, t=4),
                 live["w%d%d" % (a, lo // HALF)][:, :, lo % HALF : lo % HALF + width].rearrange("p t (c i) -> p c t i", i=4),
             )
-
-        def spread_w(a, lo, engine):
-            pair = "wg%d_%d" % (a // 2, lo)
-            if pair not in live:
-                live[pair] = rot.tile([P, 2, 4 * QUARTER], BF16, tag="w_grouped%d" % QUARTER, bufs=3, align_bytes=64, name=pair)
-            bank = psum.tile([P, 4 * QUARTER], BF16, tag="acc", name="w_ps%d_%d" % (a, lo))
-            for i in range(2):
-                first = lo % HALF + i * P
-                nc.tensor.matmul(
-                    bank[:, i * HALF : (i + 1) * HALF],
-                    lhsT=ident_bf[:],
-                    rhs=live["w%d%d" % (a, lo // HALF)][:, :, first : first + P].rearrange("p t c -> p c t"),
-                    start=True,
-                    stop=True,
-                )
-            copy_on(engine, live[pair][:, a % 2, :], bank[:])
 
         def quantise_w(g, lo):
             experts = slice(2 * g, 2 * g + 2)
@@ -260,7 +243,6 @@ def tile_expertparallelbehindblock_t_kernel(tc, inputs, combine_weights, weight,
 
         zero_bias_row()
         make_identity(nc, ident[:])
-        make_identity(nc, ident_bf[:])
         load_x(0)
         load_x(1)
         load_bias()
@@ -295,8 +277,8 @@ def tile_expertparallelbehindblock_t_kernel(tc, inputs, combine_weights, weight,
         quantise_x(1)
         stage1_bias(0, 0, 256)
         regroup_w(2, 0, 256, "v")
-        spread_w(0, 256, "s")
-        spread_w(1, 256, "v")
+        regroup_w(0, 256, 256, "s")
+        regroup_w(1, 256, 256, "v")
         transpose_cw(0)
         regroup_w(3, 0, 256, "v")
         quantise_w(1, 0)
@@ -309,7 +291,7 @@ def tile_expertparallelbehindblock_t_kernel(tc, inputs, combine_weights, weight,
         stage1_bias(1, 0, 256)
         quantise_flat(1, 0, 256)
         copy_cw(1, "sssv")
-        spread_w(2, 256, "s")
+        regroup_w(2, 256, 256, "v")
         quarter_rows(0, 0, "ss")
         quantise_w(0, 256)
         quantise_cw(1)

@@ -248,8 +248,8 @@ def tile_expertparallelbehindblock_t_kernel(tc, inputs, combine_weights, weight,
         load_bias()
         load_w(0, 0)
         load_w(1, 0)
-        load_cw(0)
         load_w(2, 0)
+        load_cw(0)
         load_w(3, 0)
         load_cw(1)
         load_cw(2)
@@ -330,14 +330,14 @@ def tile_expertparallelbehindblock_t_kernel(tc, inputs, combine_weights, weight,
         regroup_w(3, 512, 512, "v")
         quantise_w(1, 512)
         quantise_cw(5)
-        copy_cw(6, "sssv")
+        copy_cw(6, "ssss")
         stage1_passes(1, 512, 512)
-        quantise_flat(0, 512, 512)
         stage1_bias(1, 512, 512)
+        quantise_flat(0, 512, 512)
         quantise_flat(1, 512, 512)
+        half_rows(5, 0, "ssss")
         transpose_cw(7)
-        half_rows(5, 0, "ssvs")
-        copy_cw(7, "vsvs")
+        copy_cw(7, "vvvs")
         half_rows(0, 1, "vsvs")
         quantise_cw(6)
         half_rows(1, 1, "vsvs")

@@ -33,7 +33,7 @@ def tile_expertparallelbehindblock_t_kernel(tc, inputs, combine_weights, weight,
         out_rows = out.rearrange("b (h p j) d -> (b h) p j d", p=P, j=4)
 
         ident = keep.tile([P, P], F32)
-        ones = keep.tile([P, P], BF16)
+        ones = keep.tile([P, HALF], BF16)
         bias_all = keep.tile([P, 2, EXPERTS, HALF], BF16)
         x_codes = keep.tile([P, 8 * P], U32, align_bytes=64)
         x_scales = keep.tile([P, 8 * P], U8, align_bytes=64)
@@ -75,8 +75,8 @@ def tile_expertparallelbehindblock_t_kernel(tc, inputs, combine_weights, weight,
 
         def zero_bias_row():
             big_tile("bias_row", [P, EXPERTS * D_OUT], BF16)
-            nc.vector.memset(live["bias_row"][:].bitcast(I32), 0)
             nc.vector.memset(ones[:], 1.0)
+            nc.vector.memset(live["bias_row"][:].bitcast(I32), 0)
 
         def load_bias():
             nc.sync.dma_start(out=live["bias_row"][0:1, :], in_=bias.rearrange("e o d -> o (e d)"))
@@ -87,7 +87,13 @@ def tile_expertparallelbehindblock_t_kernel(tc, inputs, combine_weights, weight,
                 live["bias_ps%d%d" % (n, b)] = bank
                 for i in range(2):
                     first = (2 * b + i) * D_OUT + n * HALF
-                    nc.tensor.matmul(bank[:, i, :], lhsT=ones[:], rhs=live["bias_row"][:, first : first + HALF], start=True, stop=True)
+                    nc.tensor.matmul(bank[:, i, :], lhsT=ones[:, 0:P], rhs=live["bias_row"][:, first : first + HALF], start=True, stop=True)
+
+        def keep_warm(n):
+            live["warm"] = live.get("warm", 0) + 1
+            bank = psum.tile([P, HALF], F32, tag="acc", name="warm_ps%d" % live["warm"])
+            for i in range(n):
+                nc.tensor.matmul(bank[:], lhsT=ones[:, 0:P], rhs=ones[:], start=True, stop=True)
 
         def copy_bias(n):
             for b in range(2):
@@ -263,6 +269,7 @@ def tile_expertparallelbehindblock_t_kernel(tc, inputs, combine_weights, weight,
         load_cw(6)
         load_cw(7)
         big_tile("x_grouped", [P, 4096], BF16)
+        keep_warm(8)
         transpose_x()
         copy_x("svvs")
         quantise_x(0)
@@ -279,6 +286,7 @@ def tile_expertparallelbehindblock_t_kernel(tc, inputs, combine_weights, weight,
         regroup_w(2, 0, 256, "v")
         regroup_w(0, 256, 256, "s")
         regroup_w(1, 256, 256, "v")
+        keep_warm(2)
         transpose_cw(0)
         regroup_w(3, 0, 256, "v")
         quantise_w(1, 0)
@@ -286,17 +294,20 @@ def tile_expertparallelbehindblock_t_kernel(tc, inputs, combine_weights, weight,
         copy_cw(0, "ssss")
         quantise_cw(0)
         regroup_w(3, 256, 256, "s")
+        keep_warm(6)
         stage1_passes(1, 0, 256)
         transpose_cw(1)
         stage1_bias(1, 0, 256)
         quantise_flat(1, 0, 256)
         copy_cw(1, "sssv")
         regroup_w(2, 256, 256, "v")
+        keep_warm(2)
         quarter_rows(0, 0, "ss")
         quantise_w(0, 256)
         quantise_cw(1)
         transpose_cw(2)
         quantise_w(1, 256)
+        keep_warm(2)
         stage1_passes(0, 256, 256)
         stage1_bias(0, 256, 256)
         copy_cw(2, "ssss")

@@ -236,16 +236,25 @@ def tile_expertparallelbehindblock_t_kernel(tc, inputs, combine_weights, weight,
                     rows = slice(j + 1 - each, j + 1)
                     nc.sync.dma_start(out=out_rows[c][:, rows, n * HALF : (n + 1) * HALF], in_=o_tile[:, rows, :])
 
-        def whole_rows(c, tiles_a_store, engines="vs"):
-            for j in range(4):
+        def whole_rows(c, tiles, tiles_a_store):
+            for j in tiles:
                 if j % tiles_a_store == 0:
                     o_tile = big_tile("o%dj%d" % (c, j), [P, tiles_a_store, D_OUT], F32)
                 for n in range(2):
                     acc = psum.tile([P, HALF], F32, tag="acc", name="acc%d%d%d" % (c, j, n))
                     combine_passes(acc[:], c, j, n * HALF, HALF)
-                    copy_on(engines[n], o_tile[:, j % tiles_a_store, n * HALF : (n + 1) * HALF], acc[:])
+                    copy_on("vs"[n], o_tile[:, j % tiles_a_store, n * HALF : (n + 1) * HALF], acc[:])
                 if (j + 1) % tiles_a_store == 0:
                     nc.sync.dma_start(out=out_rows[c][:, j + 1 - tiles_a_store : j + 1, :], in_=o_tile[:])
+
+        def last_tile(c, j):
+            o_tile = big_tile("o_last", [P, D_OUT], F32)
+            for q in range(4):
+                cols = slice(q * QUARTER, (q + 1) * QUARTER)
+                acc = psum.tile([P, QUARTER], F32, tag="acc", name="acc_last%d" % q)
+                combine_passes(acc[:], c, j, q * QUARTER, QUARTER)
+                copy_on("vs"[q % 2], o_tile[:, cols], acc[:])
+                nc.sync.dma_start(out=out_rows[c][:, j, cols], in_=o_tile[:, cols])
 
         zero_bias_row()
         make_identity(nc, ident[:])
@@ -269,7 +278,7 @@ def tile_expertparallelbehindblock_t_kernel(tc, inputs, combine_weights, weight,
         load_cw(6)
         load_cw(7)
         big_tile("x_grouped", [P, 4096], BF16)
-        keep_warm(8)
+        keep_warm(4)
         transpose_x()
         copy_x("svvs")
         quantise_x(0)
@@ -357,5 +366,7 @@ def tile_expertparallelbehindblock_t_kernel(tc, inputs, combine_weights, weight,
         half_rows(3, 1, "vsvs")
         half_rows(4, 1, "vsvs")
         half_rows(5, 1, "vsvs")
-        whole_rows(6, 2)
-        whole_rows(7, 1)
+        whole_rows(6, range(4), 2)
+        whole_rows(7, range(2), 2)
+        whole_rows(7, [2], 1)
+        last_tile(7, 3)

from contextlib import ExitStack

import concourse.mybir as mybir
from concourse.masks import make_identity

F32 = mybir.dt.float32
BF16 = mybir.dt.bfloat16
I32 = mybir.dt.int32
U32 = mybir.dt.uint32
U8 = mybir.dt.uint8
FP8X4 = mybir.dt.float8_e4m3fn_x4
ADD = mybir.AluOpType.add

P = 128
EXPERTS = 4
D_IN = 512
D_OUT = 1024
QUARTER = 256
HALF = 512
SUPER_TILES = 8
FLOPS = 2 * 1024 * D_IN * D_OUT + 2 * 4096 * 1024 * D_OUT


def tile_expertparallelbehindblock_t_kernel(tc, inputs, combine_weights, weight, bias, out):
    nc = tc.nc
    with ExitStack() as ctx:
        keep = ctx.enter_context(tc.tile_pool(name="keep", bufs=1))
        rot = ctx.enter_context(tc.tile_pool(name="rot", bufs=1))
        psum = ctx.enter_context(tc.psum_pool(name="psum", bufs=4))
        ctx.enter_context(tc.manual_schedule())

        cw_rows = combine_weights.rearrange("(c p j) e k -> c p j (e k)", p=P, j=4)
        out_rows = out.rearrange("b (h p j) d -> (b h) p j d", p=P, j=4)

        ident = keep.tile([P, P], F32)
        ones = keep.tile([P, HALF], BF16)
        bias_all = keep.tile([P, 2, EXPERTS, HALF], BF16)
        x_codes = keep.tile([P, 8 * P], U32, align_bytes=64)
        x_scales = keep.tile([P, 8 * P], U8, align_bytes=64)
        w_codes, w_scales = {}, {}
        for lo, width in ((0, QUARTER), (QUARTER, QUARTER), (HALF, HALF)):
            w_codes[lo] = keep.tile([P, EXPERTS, width], U32, align_bytes=64, name="w_codes%d" % lo)
            w_scales[lo] = keep.tile([P, EXPERTS, width], U8, align_bytes=64, name="w_scales%d" % lo)
        f_codes = keep.tile([P, 2, D_OUT], U32, align_bytes=64)
        f_scales = keep.tile([P, 2, D_OUT], U8, align_bytes=64)

        live = {}

        def big_tile(name, shape, dtype):
            live[name] = rot.tile(shape, dtype, tag="big", bufs=6, align_bytes=64, name=name)
            return live[name]

        def copy_on(engine, dst, src):
            if engine == "v":
                nc.vector.tensor_copy(out=dst, in_=src)
            else:
                nc.scalar.copy(out=dst, in_=src)

        def load_x(h):
            if "x" not in live:
                big_tile("x", [P, 8, D_IN], BF16)
            nc.sync.dma_start(
                out=live["x"][:, 4 * h : 4 * h + 4, :].rearrange("p (a e) k -> p a e k", e=2),
                in_=inputs[512 * h : 512 * (h + 1), :].rearrange("(a p e) k -> p a e k", a=2, e=2),
            )

        def load_w(a, n):
            raw = rot.tile([P, 4, HALF], BF16, tag="w", bufs=6, name="w%d%d" % (a, n))
            live["w%d%d" % (a, n)] = raw
            nc.sync.dma_start(out=raw[:], in_=weight[a][:, n * HALF : (n + 1) * HALF].rearrange("(q t) d -> q t d", t=4))

        def load_cw(c):
            live["cw%d" % c] = rot.tile([P, 4, 1024], BF16, tag="cw", bufs=4, name="cw%d" % c)
            nc.sync.dma_start(out=live["cw%d" % c][:], in_=cw_rows[c])

        def zero_bias_row():
            big_tile("bias_row", [P, EXPERTS * D_OUT], BF16)
            nc.vector.memset(ones[:], 1.0)
            nc.vector.memset(live["bias_row"][:].bitcast(I32), 0)

        def load_bias():
            nc.sync.dma_start(out=live["bias_row"][0:1, :], in_=bias.rearrange("e o d -> o (e d)"))

        def spread_bias(n):
            for b in range(2):
                bank = psum.tile([P, 2, HALF], BF16, tag="acc", name="bias_ps%d%d" % (n, b))
                live["bias_ps%d%d" % (n, b)] = bank
                for i in range(2):
                    first = (2 * b + i) * D_OUT + n * HALF
                    nc.tensor.matmul(bank[:, i, :], lhsT=ones[:, 0:P], rhs=live["bias_row"][:, first : first + HALF], start=True, stop=True)

        def keep_warm(n):
            live["warm"] = live.get("warm", 0) + 1
            bank = psum.tile([P, HALF], F32, tag="acc", name="warm_ps%d" % live["warm"])
            for i in range(n):
                nc.tensor.matmul(bank[:], lhsT=ones[:, 0:P], rhs=ones[:], start=True, stop=True)

        def copy_bias(n):
            for b in range(2):
                nc.scalar.copy(out=bias_all[:, n, 2 * b : 2 * b + 2, :], in_=live["bias_ps%d%d" % (n, b)][:])

        def transpose_x():
            words = live["x"][:].bitcast(F32)
            for i in range(4):
                bank = psum.tile([P, 2, 2, P], F32, tag="tr", name="x_ps%d" % i)
                live["x_ps%d" % i] = bank
                for i2 in range(2):
                    for u in range(2):
                        nc.tensor.transpose(bank[:, i2, u, :], words[:, 2 * i + i2, u : D_IN // 2 : 2], ident[:])

        def copy_x(engines):
            words = live["x_grouped"][:].bitcast(F32).rearrange("p (i s u) -> p i s u", i=8, u=2)
            for i in range(4):
                copy_on(engines[i], words[:, 2 * i : 2 * i + 2, :, :], live["x_ps%d" % i][:].rearrange("p i u s -> p i s u"))

        def quantise_x(g):
            nc.vector.quantize_mx(
                out=x_codes[:, g * 512 : (g + 1) * 512].bitcast(FP8X4),
                scales=x_scales[:, g * 512 : (g + 1) * 512],
                in_=live["x_grouped"][:, g * 2048 : (g + 1) * 2048],
            )

        def regroup_w(a, lo, width, engine):
            pair = "wg%d_%d" % (a // 2, lo)
            if pair not in live:
                live[pair] = rot.tile([P, 2, 4 * width], BF16, tag="w_grouped%d" % width, bufs=3 if width == QUARTER else 1, align_bytes=64, name=pair)
            copy_on(
                engine,
                live[pair][:, a % 2, :].rearrange("p (c i t) -> p c t i", i=4, t=4),
                live["w%d%d" % (a, lo // HALF)][:, :, lo % HALF : lo % HALF + width].rearrange("p t (c i) -> p c t i", i=4),
            )

        def quantise_w(g, lo):
            experts = slice(2 * g, 2 * g + 2)
            nc.vector.quantize_mx(
                out=w_codes[lo][:, experts, :].rearrange("p a d -> p (a d)").bitcast(FP8X4),
                scales=w_scales[lo][:, experts, :].rearrange("p a d -> p (a d)"),
                in_=live["wg%d_%d" % (g, lo)][:].rearrange("p a k -> p (a k)"),
            )

        def stage1_passes(g, lo, width):
            for d in range(lo // P, (lo + width) // P):
                cols = slice(d * P - lo, (d + 1) * P - lo)
                bank = psum.tile([P, 2, 2, P], F32, tag="acc", name="f_ps%d%d" % (g, d))
                live["f_ps%d%d" % (g, d)] = bank
                for u in range(2):
                    a = 2 * g + u
                    for e in range(2):
                        slots = slice((2 * a + e) * P, (2 * a + e + 1) * P)
                        nc.tensor.matmul_mx(
                            out=bank[:, u, e, :],
                            lhsT=x_codes[:, slots].bitcast(FP8X4),
                            lhsT_scale=x_scales[:, slots],
                            rhs=w_codes[lo][:, a, cols].bitcast(FP8X4),
                            rhs_scale=w_scales[lo][:, a, cols],
                            start=True,
                            stop=True,
                        )

        def stage1_bias(g, lo, width):
            grouped = rot.tile([P, width, 4], BF16, tag="f_grouped%d" % width, bufs=2, align_bytes=64, name="fg%d_%d" % (g, lo))
            live["fg%d_%d" % (g, lo)] = grouped
            for i in range(width // P):
                d = lo // P + i
                b_view = bias_all[:, d // 4, 2 * g : 2 * g + 2, d % 4 * P : (d % 4 + 1) * P].rearrange("p u d -> p d u").unsqueeze(3)
                nc.vector.tensor_tensor(
                    out=grouped[:, i * P : (i + 1) * P, :].rearrange("p d (u e) -> p d u e", e=2),
                    in0=live["f_ps%d%d" % (g, d)][:].rearrange("p u e d -> p d u e"),
                    in1=b_view.to_broadcast([P, P, 2, 2]),
                    op=ADD,
                )

        def quantise_flat(g, lo, width):
            cols = slice(lo, lo + width)
            nc.vector.quantize_mx(
                out=f_codes[:, g, cols].bitcast(FP8X4),
                scales=f_scales[:, g, cols],
                in_=live["fg%d_%d" % (g, lo)][:].rearrange("p d t -> p (d t)"),
            )

        def transpose_cw(c):
            words = live["cw%d" % c][:].bitcast(F32)
            for j in range(4):
                bank = psum.tile([P, 4, P], F32, tag="tr", name="cw_ps%d%d" % (c, j))
                live["cw_ps%d%d" % (c, j)] = bank
                for a in range(4):
                    nc.tensor.transpose(bank[:, a, :], words[:, j, a * P : (a + 1) * P], ident[:])

        def copy_cw(c, engines):
            live["cwg%d" % c] = rot.tile([P, 4096], BF16, tag="cw_grouped", bufs=2, align_bytes=64, name="cwg%d" % c)
            words = live["cwg%d" % c][:].bitcast(F32).rearrange("p (j g s u) -> p j g s u", j=4, g=2, u=2)
            for j in range(4):
                copy_on(engines[j], words[:, j], live["cw_ps%d%d" % (c, j)][:].rearrange("p (g u) s -> p g s u", u=2))

        def quantise_cw(c):
            live["cwq%d" % c] = rot.tile([P, 1024], U32, tag="cw_codes", bufs=7, align_bytes=64, name="cwq%d" % c)
            live["cws%d" % c] = rot.tile([P, 1024], U8, tag="cw_scales", bufs=7, align_bytes=64, name="cws%d" % c)
            nc.vector.quantize_mx(
                out=live["cwq%d" % c][:].bitcast(FP8X4), scales=live["cws%d" % c][:], in_=live["cwg%d" % c][:]
            )

        def combine_passes(acc, c, j, lo, width):
            for g in range(2):
                rows = slice((2 * j + g) * P, (2 * j + g + 1) * P)
                nc.tensor.matmul_mx(
                    out=acc,
                    lhsT=live["cwq%d" % c][:, rows].bitcast(FP8X4),
                    lhsT_scale=live["cws%d" % c][:, rows],
                    rhs=f_codes[:, g, lo : lo + width].bitcast(FP8X4),
                    rhs_scale=f_scales[:, g, lo : lo + width],
                    start=(g == 0),
                    stop=(g == 1),
                )

        def quarter_rows(c, q, engines):
            n = q // 2
            if q % 2 == 0:
                big_tile("o%dn%d" % (c, n), [P, 4, HALF], F32)
            o_tile = live["o%dn%d" % (c, n)]
            for i in range(2):
                bank = psum.tile([P, 2, QUARTER], F32, tag="acc", name="acc%dq%d%d" % (c, q, i))
                for j in range(2):
                    combine_passes(bank[:, j, :], c, 2 * i + j, q * QUARTER, QUARTER)
                copy_on(engines[i], o_tile[:, 2 * i : 2 * i + 2, (q % 2) * QUARTER : (q % 2 + 1) * QUARTER], bank[:])
            if q % 2 == 1:
                nc.sync.dma_start(out=out_rows[c][:, :, n * HALF : (n + 1) * HALF], in_=o_tile[:])

        def half_rows(c, n, engines, parts=1):
            o_tile = big_tile("o%dn%d" % (c, n), [P, 4, HALF], F32)
            each = 4 // parts
            for j in range(4):
                acc = psum.tile([P, HALF], F32, tag="acc", name="acc%d%d%d" % (c, j, n))
                combine_passes(acc[:], c, j, n * HALF, HALF)
                copy_on(engines[j], o_tile[:, j, :], acc[:])
                if (j + 1) % each == 0:
                    rows = slice(j + 1 - each, j + 1)
                    nc.sync.dma_start(out=out_rows[c][:, rows, n * HALF : (n + 1) * HALF], in_=o_tile[:, rows, :])

        def whole_rows(c, tiles, tiles_a_store):
            for j in tiles:
                if j % tiles_a_store == 0:
                    o_tile = big_tile("o%dj%d" % (c, j), [P, tiles_a_store, D_OUT], F32)
                for n in range(2):
                    acc = psum.tile([P, HALF], F32, tag="acc", name="acc%d%d%d" % (c, j, n))
                    combine_passes(acc[:], c, j, n * HALF, HALF)
                    copy_on("vs"[n], o_tile[:, j % tiles_a_store, n * HALF : (n + 1) * HALF], acc[:])
                if (j + 1) % tiles_a_store == 0:
                    nc.sync.dma_start(out=out_rows[c][:, j + 1 - tiles_a_store : j + 1, :], in_=o_tile[:])

        def last_tile(c, j):
            o_tile = big_tile("o_last", [P, D_OUT], F32)
            for q in range(4):
                cols = slice(q * QUARTER, (q + 1) * QUARTER)
                acc = psum.tile([P, QUARTER], F32, tag="acc", name="acc_last%d" % q)
                combine_passes(acc[:], c, j, q * QUARTER, QUARTER)
                copy_on("vs"[q % 2], o_tile[:, cols], acc[:])
                nc.sync.dma_start(out=out_rows[c][:, j, cols], in_=o_tile[:, cols])

        zero_bias_row()
        make_identity(nc, ident[:])
        load_x(0)
        load_x(1)
        load_bias()
        load_w(0, 0)
        load_w(1, 0)
        load_w(2, 0)
        load_cw(0)
        load_w(3, 0)
        load_cw(1)
        load_cw(2)
        load_cw(3)
        load_w(0, 1)
        load_w(1, 1)
        load_cw(4)
        load_w(2, 1)
        load_w(3, 1)
        load_cw(5)
        load_cw(6)
        load_cw(7)
        big_tile("x_grouped", [P, 4096], BF16)
        keep_warm(4)
        transpose_x()
        copy_x("svvs")
        quantise_x(0)
        spread_bias(0)
        spread_bias(1)
        regroup_w(0, 0, 256, "v")
        regroup_w(1, 0, 256, "v")
        quantise_w(0, 0)
        stage1_passes(0, 0, 256)
        copy_bias(0)
        copy_bias(1)
        quantise_x(1)
        stage1_bias(0, 0, 256)
        regroup_w(2, 0, 256, "v")
        regroup_w(0, 256, 256, "s")
        regroup_w(1, 256, 256, "v")
        keep_warm(2)
        transpose_cw(0)
        regroup_w(3, 0, 256, "v")
        quantise_w(1, 0)
        quantise_flat(0, 0, 256)
        copy_cw(0, "ssss")
        quantise_cw(0)
        regroup_w(3, 256, 256, "s")
        keep_warm(6)
        stage1_passes(1, 0, 256)
        transpose_cw(1)
        stage1_bias(1, 0, 256)
        quantise_flat(1, 0, 256)
        copy_cw(1, "sssv")
        regroup_w(2, 256, 256, "v")
        keep_warm(2)
        quarter_rows(0, 0, "ss")
        quantise_w(0, 256)
        quantise_cw(1)
        transpose_cw(2)
        quantise_w(1, 256)
        keep_warm(2)
        stage1_passes(0, 256, 256)
        stage1_bias(0, 256, 256)
        copy_cw(2, "ssss")
        transpose_cw(3)
        quantise_cw(2)
        stage1_passes(1, 256, 256)
        copy_cw(3, "ssss")
        stage1_bias(1, 256, 256)
        quarter_rows(1, 0, "ss")
        quarter_rows(2, 0, "ss")
        transpose_cw(4)
        quantise_flat(0, 256, 256)
        quantise_flat(1, 256, 256)
        regroup_w(0, 512, 512, "v")
        regroup_w(1, 512, 512, "v")
        quantise_cw(3)
        copy_cw(4, "sssv")
        quarter_rows(0, 1, "ss")
        quarter_rows(1, 1, "ss")
        quantise_w(0, 512)
        quantise_cw(4)
        half_rows(3, 0, "ssss")
        transpose_cw(5)
        copy_cw(5, "ssss")
        regroup_w(2, 512, 512, "v")
        stage1_passes(0, 512, 512)
        half_rows(4, 0, "ssss")
        quarter_rows(2, 1, "ss")
        transpose_cw(6)
        stage1_bias(0, 512, 512)
        regroup_w(3, 512, 512, "v")
        quantise_w(1, 512)
        quantise_cw(5)
        copy_cw(6, "ssss")
        stage1_passes(1, 512, 512)
        stage1_bias(1, 512, 512)
        quantise_flat(0, 512, 512)
        quantise_flat(1, 512, 512)
        half_rows(5, 0, "ssss")
        transpose_cw(7)
        copy_cw(7, "vvvs")
        half_rows(0, 1, "vsvs")
        quantise_cw(6)
        half_rows(1, 1, "vsvs")
        quantise_cw(7)
        half_rows(2, 1, "vsvs")
        half_rows(3, 1, "vsvs")
        half_rows(4, 1, "vsvs")
        half_rows(5, 1, "vsvs")
        whole_rows(6, range(4), 2)
        whole_rows(7, range(2), 2)
        whole_rows(7, [2], 1)
        last_tile(7, 3)
